import numpy as np
import ml_dtypes


def mxq(x, axis, fmt="e4m3"):
    dtype, down = {"e4m3": (ml_dtypes.float8_e4m3fn, 7), "e5m2": (ml_dtypes.float8_e5m2, 14)}[fmt]
    v = np.moveaxis(np.asarray(x, np.float32).astype(ml_dtypes.bfloat16).astype(np.float64), axis, -1)
    blocks = v.reshape(v.shape[:-1] + (-1, 32))
    amax = np.abs(blocks).max(-1, keepdims=True)
    byte = np.maximum(np.where(amax > 0, np.frexp(amax)[1] - 1 + 127, 0) - down, 1)
    scale = np.exp2(byte - 127.0)
    codes = (blocks / scale).astype(np.float32).astype(dtype).astype(np.float64)
    return np.moveaxis((codes * scale).reshape(v.shape), -1, axis)


WIDE = False


def mx_kscale(k):
    if not WIDE:
        return np.ones(k)
    levels = np.array([10, -10, 5, -5, 0])
    a = np.random.permutation(np.resize(levels, k // 512 * 4)).reshape(k // 512, 4)
    idx = np.arange(k)
    return np.exp2(a[idx // 512, idx % 128 // 32])


BF16 = ml_dtypes.bfloat16


def bf(x):
    return np.asarray(x, np.float32).astype(BF16)


def f64(x):
    return np.asarray(x).astype(np.float64)


B, S, HIDDEN, Q_LORA, NUM_HEADS, QK_NOPE, QK_ROPE, KV_LORA = 2, 2048, 1024, 512, 2, 128, 64, 192
QK_HEAD = QK_NOPE + QK_ROPE


def rotate_half(t):
    d = t.shape[-1] // 2
    return np.concatenate([-t[..., d:], t[..., :d]], axis=-1)


def setup_inputs():
    s, t = mx_kscale(HIDDEN), mx_kscale(Q_LORA)
    x = bf(np.random.standard_normal((B, S, HIDDEN)) * s)
    cos = bf(np.random.uniform(size=(B, S, QK_ROPE)))
    sin = bf(np.random.uniform(size=(B, S, QK_ROPE)))
    Wqa = bf(np.random.standard_normal((Q_LORA, HIDDEN)) / np.sqrt(HIDDEN) * t[:, None] / s)
    Wqb = bf(np.random.standard_normal((NUM_HEADS * QK_HEAD, Q_LORA)) / np.sqrt(Q_LORA) / t)
    Wkva = bf(np.random.standard_normal((KV_LORA + QK_ROPE, HIDDEN)) / np.sqrt(HIDDEN) / s)
    return {"x": x, "cos": cos, "sin": sin, "Wqa": Wqa, "Wqb": Wqb, "Wkva": Wkva}


def reference(x, cos, sin, Wqa, Wqb, Wkva):
    b, s, _ = x.shape
    xq = mxq(f64(x), 2, "e4m3")
    qa = xq @ mxq(f64(Wqa), 1, "e4m3").T
    q = (mxq(qa, 2, "e4m3") @ mxq(f64(Wqb), 1, "e4m3").T).reshape(b, s, NUM_HEADS, QK_HEAD)
    q_nope = q[..., :QK_NOPE]
    q_pe = q[..., QK_NOPE:]
    kv = xq @ mxq(f64(Wkva), 1, "e4m3").T
    compressed_kv = kv[..., :KV_LORA]
    k_pe = kv[..., KV_LORA:].reshape(b, s, 1, QK_ROPE)
    c = f64(cos)[:, :, None, :]
    sn = f64(sin)[:, :, None, :]
    q_pe_rot = q_pe * c + rotate_half(q_pe) * sn
    k_pe_rot = k_pe * c + rotate_half(k_pe) * sn
    q_out = np.concatenate([q_nope, q_pe_rot], axis=-1).reshape(b, s, -1)
    k_out = k_pe_rot.reshape(b, s, QK_ROPE)
    return np.concatenate([q_out, k_out, compressed_kv], axis=-1)

@@ -1,0 +1,292 @@
+from contextlib import ExitStack
+
+import concourse.mybir as mybir
+from concourse.masks import make_identity
+
+F32 = mybir.dt.float32
+BF16 = mybir.dt.bfloat16
+U32 = mybir.dt.uint32
+U8 = mybir.dt.uint8
+FP8X4 = mybir.dt.float8_e4m3fn_x4
+MULT = mybir.AluOpType.mult
+ADD = mybir.AluOpType.add
+SUB = mybir.AluOpType.subtract
+
+P = 128
+TOKENS = 4096
+HIDDEN = 1024
+Q_LORA = 512
+ROUNDS = 8
+TILES = 4
+OUT_W = 640
+
+FLOPS = 2 * TOKENS * (HIDDEN * 768 + Q_LORA * 384)
+
+PIN = True
+
+
+def tile_mlaselfattn_t_kernel(tc, x, cos, sin, Wqa, Wqb, Wkva, out):
+    nc = tc.nc
+    with ExitStack() as ctx:
+        if PIN:
+            ctx.enter_context(tc.manual_schedule())
+        const = ctx.enter_context(tc.tile_pool(name="const", bufs=1))
+        xpool = ctx.enter_context(tc.tile_pool(name="xpool", bufs=ROUNDS))
+        xgp = ctx.enter_context(tc.tile_pool(name="xgp", bufs=4))
+        xcp = ctx.enter_context(tc.tile_pool(name="xcp", bufs=6))
+        qgp = ctx.enter_context(tc.tile_pool(name="qgp", bufs=4))
+        qcp = ctx.enter_context(tc.tile_pool(name="qcp", bufs=8))
+        outp = ctx.enter_context(tc.tile_pool(name="outp", bufs=3))
+        tmpp = ctx.enter_context(tc.tile_pool(name="tmpp", bufs=2))
+        psum = ctx.enter_context(tc.psum_pool(name="psum", bufs=8))
+
+        xv = x.flatten_outer_dims().rearrange("(p r i) k -> p r (i k)", p=P, r=ROUNDS, i=TILES)
+        ov = out.flatten_outer_dims().rearrange("(p r i) c -> p r (i c)", p=P, r=ROUNDS, i=TILES)
+        cosv = cos.flatten_outer_dims().rearrange("(p t) c -> p (t c)", p=P)
+        sinv = sin.flatten_outer_dims().rearrange("(p t) c -> p (t c)", p=P)
+
+        wqa_raw = const.tile([P, 4, HIDDEN], BF16, name="wqa_raw", tag="wqa_raw")
+        wkv_raw = const.tile([P, 2, HIDDEN], BF16, name="wkv_raw", tag="wkv_raw")
+        wqb_raw = const.tile([P, 3, Q_LORA], BF16, name="wqb_raw", tag="wqb_raw")
+        cos_sb = const.tile([P, 32, 64], BF16, name="cos_sb", tag="cos_sb")
+        sin_sb = const.tile([P, 32, 64], BF16, name="sin_sb", tag="sin_sb")
+        sinx = const.tile([P, 32, 64], BF16, name="sinx", tag="sinx")
+        ident = const.tile([P, P], F32, name="ident", tag="ident")
+        x_sb = [xpool.tile([P, TILES, HIDDEN], BF16, name="x%d" % r, tag="x") for r in range(ROUNDS)]
+
+        make_identity(nc, ident[:])
+
+        wqa_v = Wqa.rearrange("(u p e) k -> p u (e k)", u=2, p=P, e=2)
+        for u in range(2):
+            nc.sync.dma_start(
+                out=wqa_raw[:, 2 * u : 2 * u + 2, :].rearrange("p e k -> p (e k)"), in_=wqa_v[:, u, :]
+            )
+        for h in range(2):
+            nc.sync.dma_start(
+                out=x_sb[0][:, 2 * h : 2 * h + 2, :].rearrange("p i k -> p (i k)"),
+                in_=xv[:, 0, 2 * h * HIDDEN : (2 * h + 2) * HIDDEN],
+            )
+        nc.sync.dma_start(out=wkv_raw[:], in_=Wkva.rearrange("(b p) k -> p b k", p=P))
+        nc.sync.dma_start(out=wqb_raw[:, 0:2, :], in_=Wqb.rearrange("(h r) k -> r h k", h=2)[0:128, :, :])
+        nc.sync.dma_start(out=wqb_raw[0:64, 2, :], in_=Wqb[128:192, :])
+        nc.sync.dma_start(out=wqb_raw[64:128, 2, :], in_=Wqb[320:384, :])
+        nc.sync.dma_start(out=x_sb[1][:].rearrange("p i k -> p (i k)"), in_=xv[:, 1, :])
+        nc.sync.dma_start(out=cos_sb[:].rearrange("p t c -> p (t c)"), in_=cosv)
+        nc.sync.dma_start(out=sin_sb[:].rearrange("p t c -> p (t c)"), in_=sinv)
+        for r in range(2, ROUNDS):
+            nc.sync.dma_start(out=x_sb[r][:].rearrange("p i k -> p (i k)"), in_=xv[:, r, :])
+
+        def new_bank(nm):
+            return psum.tile([P, 512], F32, name=nm, tag="bank")
+
+        def transpose_bank(nm, blocks, g):
+            n = len(blocks) * P
+            bank = new_bank(nm)
+            for u in range(2):
+                for b in range(len(blocks)):
+                    w0 = 256 * g + 128 * u
+                    nc.tensor.transpose(
+                        out=bank[:, u * n + b * P : u * n + (b + 1) * P],
+                        in_=blocks[b].bitcast(F32)[:, w0 : w0 + P],
+                        identity=ident[:],
+                    )
+            return bank[:, 0 : 2 * n].rearrange("p (u n) -> p n u", u=2)
+
+        def drain_words(eng_is_scalar, grouped2d, src):
+            dst = grouped2d.bitcast(F32).rearrange("p (n u) -> p n u", u=2)
+            if eng_is_scalar:
+                nc.scalar.copy(out=dst, in_=src)
+            else:
+                nc.vector.tensor_copy(out=dst, in_=src)
+
+        def quant(codes, scales, grouped2d):
+            nc.vector.quantize_mx(out=codes.bitcast(FP8X4), scales=scales, in_=grouped2d)
+
+        def mx(o, l, ls, r_, rs, start, stop):
+            nc.tensor.matmul_mx(
+                out=o, lhsT=l.bitcast(FP8X4), lhsT_scale=ls, rhs=r_.bitcast(FP8X4), rhs_scale=rs,
+                start=start, stop=stop,
+            )
+
+        wqa_g = const.tile([P, 2, 512, 4], BF16, name="wqa_g", tag="wqa_g", align_bytes=64)
+        wqa_c = const.tile([P, 2, 512], U32, name="wqa_c", tag="wqa_c", align_bytes=64)
+        wqa_s = const.tile([P, 2, 512], U8, name="wqa_s", tag="wqa_s", align_bytes=64)
+        wkv_g = const.tile([P, 2, 256, 4], BF16, name="wkv_g", tag="wkv_g", align_bytes=64)
+        wkv_c = const.tile([P, 2, 256], U32, name="wkv_c", tag="wkv_c", align_bytes=64)
+        wkv_s = const.tile([P, 2, 256], U8, name="wkv_s", tag="wkv_s", align_bytes=64)
+        wqb_g = const.tile([P, 384, 4], BF16, name="wqb_g", tag="wqb_g", align_bytes=64)
+        wqb_c = const.tile([P, 384], U32, name="wqb_c", tag="wqb_c", align_bytes=64)
+        wqb_s = const.tile([P, 384], U8, name="wqb_s", tag="wqb_s", align_bytes=64)
+
+        def prep_wqa():
+            k = 0
+            for jp in range(2):
+                for g in range(2):
+                    src = transpose_bank("wa%d%d" % (jp, g), [wqa_raw[:, 2 * jp, :], wqa_raw[:, 2 * jp + 1, :]], g)
+                    drain_words(k % 2 == 0, wqa_g[:, g, 256 * jp : 256 * jp + 256, :].rearrange("p n t -> p (n t)"), src)
+                    k += 1
+            for g in range(2):
+                quant(wqa_c[:, g, :], wqa_s[:, g, :], wqa_g[:, g, :, :].rearrange("p n t -> p (n t)"))
+
+        def prep_wkv():
+            for g in range(2):
+                src = transpose_bank("wk%d" % g, [wkv_raw[:, 0, :], wkv_raw[:, 1, :]], g)
+                drain_words(g == 0, wkv_g[:, g, :, :].rearrange("p n t -> p (n t)"), src)
+            quant(
+                wkv_c[:].rearrange("p g n -> p (g n)"),
+                wkv_s[:].rearrange("p g n -> p (g n)"),
+                wkv_g[:].rearrange("p g n t -> p (g n t)"),
+            )
+
+        def prep_wqb():
+            src = transpose_bank("wb0", [wqb_raw[:, 0, :], wqb_raw[:, 1, :]], 0)
+            drain_words(True, wqb_g[:, 0:256, :].rearrange("p n t -> p (n t)"), src)
+            src = transpose_bank("wb1", [wqb_raw[:, 2, :]], 0)
+            drain_words(False, wqb_g[:, 256:384, :].rearrange("p n t -> p (n t)"), src)
+            quant(wqb_c[:, 0:256], wqb_s[:, 0:256], wqb_g[:, 0:256, :].rearrange("p n t -> p (n t)"))
+            quant(wqb_c[:, 256:384], wqb_s[:, 256:384], wqb_g[:, 256:384, :].rearrange("p n t -> p (n t)"))
+
+        xc = {}
+        xs = {}
+        qc = {}
+        qs = {}
+        kbank = {}
+        nbank = {}
+        pbank = {}
+        osb = {}
+        tk = {}
+
+        def stage_x(r, both_engines):
+            grouped = []
+            for pr in range(2):
+                xg = xgp.tile([P, 2, 256, 4], BF16, name="xg%d_%d" % (r, pr), tag="xg", align_bytes=64)
+                grouped.append(xg)
+                for g in range(2):
+                    src = transpose_bank(
+                        "xt%d_%d%d" % (r, pr, g), [x_sb[r][:, 2 * pr, :], x_sb[r][:, 2 * pr + 1, :]], g
+                    )
+                    drain_words((not both_engines) or g == 0, xg[:, g, :, :].rearrange("p n t -> p (n t)"), src)
+            for pr in range(2):
+                xc[(r, pr)] = xcp.tile([P, 2, 256], U32, name="xc%d_%d" % (r, pr), tag="xc", align_bytes=64)
+                xs[(r, pr)] = xcp.tile([P, 2, 256], U8, name="xs%d_%d" % (r, pr), tag="xs", align_bytes=64)
+                quant(
+                    xc[(r, pr)][:].rearrange("p g n -> p (g n)"),
+                    xs[(r, pr)][:].rearrange("p g n -> p (g n)"),
+                    grouped[pr][:].rearrange("p g n t -> p (g n t)"),
+                )
+
+        def stage_qa(r, i):
+            pr, i2 = i // 2, i % 2
+            cols = slice(i2 * P, (i2 + 1) * P)
+            bank = new_bank("qa%d_%d" % (r, i))
+            for j in range(4):
+                for g in range(2):
+                    mx(
+                        bank[:, j * P : (j + 1) * P],
+                        wqa_c[:, g, j * P : (j + 1) * P], wqa_s[:, g, j * P : (j + 1) * P],
+                        xc[(r, pr)][:, g, cols], xs[(r, pr)][:, g, cols],
+                        g == 0, g == 1,
+                    )
+            qg = qgp.tile([P, P, 4], BF16, name="qg%d_%d" % (r, i), tag="qg", align_bytes=64)
+            nc.scalar.copy(out=qg[:], in_=bank[:].rearrange("p (j n) -> p n j", j=4))
+            return qg
+
+        def quant_qa(r, i, qg):
+            qc[(r, i)] = qcp.tile([P, P], U32, name="qc%d_%d" % (r, i), tag="qc", align_bytes=64)
+            qs[(r, i)] = qcp.tile([P, P], U8, name="qs%d_%d" % (r, i), tag="qs", align_bytes=64)
+            quant(qc[(r, i)][:], qs[(r, i)][:], qg[:].rearrange("p n t -> p (n t)"))
+
+        def pe_kv(r, pr):
+            bank = new_bank("kv%d_%d" % (r, pr))
+            kbank[(r, pr)] = bank
+            for i2 in range(2):
+                cols = slice(i2 * P, (i2 + 1) * P)
+                for g in range(2):
+                    mx(
+                        bank[:, i2 * 256 : (i2 + 1) * 256],
+                        xc[(r, pr)][:, g, cols], xs[(r, pr)][:, g, cols],
+                        wkv_c[:, g, :], wkv_s[:, g, :],
+                        g == 0, g == 1,
+                    )
+
+        def pe_q(r):
+            pbank[r] = None
+            for pr in range(2):
+                nbank[(r, pr)] = new_bank("qn%d_%d" % (r, pr))
+                if pr == 0:
+                    pbank[r] = new_bank("qp%d" % r)
+                for i2 in range(2):
+                    i = 2 * pr + i2
+                    mx(
+                        nbank[(r, pr)][:, i2 * 256 : (i2 + 1) * 256],
+                        qc[(r, i)][:], qs[(r, i)][:], wqb_c[:, 0:256], wqb_s[:, 0:256], True, True,
+                    )
+                    mx(
+                        pbank[r][:, i * P : (i + 1) * P],
+                        qc[(r, i)][:], qs[(r, i)][:], wqb_c[:, 256:384], wqb_s[:, 256:384], True, True,
+                    )
+
+        def v_kv(r, pr):
+            kv = kbank[(r, pr)][:].rearrange("p (i c) -> p i c", i=2)
+            o = osb[r]
+            t0 = TILES * r + 2 * pr
+            rows = slice(2 * pr, 2 * pr + 2)
+            nc.vector.tensor_tensor(out=o[:, rows, 384:448], in0=kv[:, :, 192:256], in1=cos_sb[:, t0 : t0 + 2, :], op=MULT)
+            nc.vector.tensor_tensor(out=tk[r][:, rows, :], in0=kv[:, :, 192:256], in1=sinx[:, t0 : t0 + 2, :], op=MULT)
+            nc.vector.tensor_copy(out=o[:, rows, 448:640], in_=kv[:, :, 0:192])
+
+        def s_nope(r, pr):
+            o = osb[r][:, 2 * pr : 2 * pr + 2, 0:384].rearrange("p i (h c) -> p i h c", h=2)
+            nc.scalar.copy(out=o[:, :, :, 0:128], in_=nbank[(r, pr)][:].rearrange("p (i h c) -> p i h c", i=2, h=2))
+
+        def v_rope(r):
+            o = osb[r]
+            oq = o[:, :, 0:384].rearrange("p i (h c) -> p i h c", h=2)
+            pe = pbank[r][:].rearrange("p (i h c) -> p i h c", i=4, h=2)
+            t0 = TILES * r
+            cb = cos_sb[:, t0 : t0 + 4, :].unsqueeze(2).to_broadcast([P, 4, 2, 64])
+            sb = sinx[:, t0 : t0 + 4, :].unsqueeze(2).to_broadcast([P, 4, 2, 64])
+            tq = tmpp.tile([P, 4, 2, 64], F32, name="tq%d" % r, tag="tq")
+            nc.vector.tensor_tensor(out=oq[:, :, :, 128:192], in0=pe, in1=cb, op=MULT)
+            nc.vector.tensor_tensor(out=tq[:], in0=pe, in1=sb, op=MULT)
+            nc.vector.tensor_tensor(out=o[:, :, 384:416], in0=o[:, :, 384:416], in1=tk[r][:, :, 32:64], op=SUB)
+            nc.vector.tensor_tensor(out=o[:, :, 416:448], in0=o[:, :, 416:448], in1=tk[r][:, :, 0:32], op=ADD)
+            nc.vector.tensor_tensor(out=oq[:, :, :, 128:160], in0=oq[:, :, :, 128:160], in1=tq[:, :, :, 32:64], op=SUB)
+            nc.vector.tensor_tensor(out=oq[:, :, :, 160:192], in0=oq[:, :, :, 160:192], in1=tq[:, :, :, 0:32], op=ADD)
+
+        def store(r):
+            nc.sync.dma_start(out=ov[:, r, :], in_=osb[r][:].rearrange("p i c -> p (i c)"))
+
+        prep_wqa()
+        stage_x(0, True)
+        for r in range(ROUNDS):
+            qg0 = stage_qa(r, 0)
+            qg1 = stage_qa(r, 1)
+            if r > 0:
+                v_rope(r - 1)
+                store(r - 1)
+            quant_qa(r, 0, qg0)
+            quant_qa(r, 1, qg1)
+            if r == 0:
+                prep_wkv()
+                prep_wqb()
+            if r + 1 < ROUNDS:
+                stage_x(r + 1, r == 0)
+            qg2 = stage_qa(r, 2)
+            quant_qa(r, 2, qg2)
+            qg3 = stage_qa(r, 3)
+            quant_qa(r, 3, qg3)
+            pe_kv(r, 0)
+            pe_kv(r, 1)
+            pe_q(r)
+            osb[r] = outp.tile([P, TILES, OUT_W], F32, name="o%d" % r, tag="o")
+            tk[r] = tmpp.tile([P, TILES, 64], F32, name="tk%d" % r, tag="tk")
+            if r == 0:
+                nc.vector.tensor_copy(out=sinx[:, :, 0:32], in_=sin_sb[:, :, 32:64])
+                nc.vector.tensor_copy(out=sinx[:, :, 32:64], in_=sin_sb[:, :, 0:32])
+            v_kv(r, 0)
+            v_kv(r, 1)
+            s_nope(r, 0)
+            s_nope(r, 1)
+        v_rope(ROUNDS - 1)
+        store(ROUNDS - 1)

@@ -22,59 +22,63 @@ OUT_W = 640
 
 FLOPS = 2 * TOKENS * (HIDDEN * 768 + Q_LORA * 384)
 
-PIN = True
-
 
 def tile_mlaselfattn_t_kernel(tc, x, cos, sin, Wqa, Wqb, Wkva, out):
     nc = tc.nc
     with ExitStack() as ctx:
-        if PIN:
-            ctx.enter_context(tc.manual_schedule())
+        ctx.enter_context(tc.manual_schedule())
         const = ctx.enter_context(tc.tile_pool(name="const", bufs=1))
         xpool = ctx.enter_context(tc.tile_pool(name="xpool", bufs=ROUNDS))
-        xgp = ctx.enter_context(tc.tile_pool(name="xgp", bufs=4))
+        xgp = ctx.enter_context(tc.tile_pool(name="xgp", bufs=6))
         xcp = ctx.enter_context(tc.tile_pool(name="xcp", bufs=6))
         qgp = ctx.enter_context(tc.tile_pool(name="qgp", bufs=4))
-        qcp = ctx.enter_context(tc.tile_pool(name="qcp", bufs=8))
-        outp = ctx.enter_context(tc.tile_pool(name="outp", bufs=3))
-        tmpp = ctx.enter_context(tc.tile_pool(name="tmpp", bufs=2))
+        qcp = ctx.enter_context(tc.tile_pool(name="qcp", bufs=10))
+        outp = ctx.enter_context(tc.tile_pool(name="outp", bufs=4))
+        tmpp = ctx.enter_context(tc.tile_pool(name="tmpp", bufs=3))
         psum = ctx.enter_context(tc.psum_pool(name="psum", bufs=8))
 
         xv = x.flatten_outer_dims().rearrange("(p r i) k -> p r (i k)", p=P, r=ROUNDS, i=TILES)
-        ov = out.flatten_outer_dims().rearrange("(p r i) c -> p r (i c)", p=P, r=ROUNDS, i=TILES)
+        ov = out.flatten_outer_dims().rearrange("(p r i) c -> p r i c", p=P, r=ROUNDS, i=TILES)
         cosv = cos.flatten_outer_dims().rearrange("(p t) c -> p (t c)", p=P)
         sinv = sin.flatten_outer_dims().rearrange("(p t) c -> p (t c)", p=P)
+        wqa_v = Wqa.rearrange("(u p e) k -> p u (e k)", u=2, p=P, e=2)
 
         wqa_raw = const.tile([P, 4, HIDDEN], BF16, name="wqa_raw", tag="wqa_raw")
         wkv_raw = const.tile([P, 2, HIDDEN], BF16, name="wkv_raw", tag="wkv_raw")
         wqb_raw = const.tile([P, 3, Q_LORA], BF16, name="wqb_raw", tag="wqb_raw")
         cos_sb = const.tile([P, 32, 64], BF16, name="cos_sb", tag="cos_sb")
         sin_sb = const.tile([P, 32, 64], BF16, name="sin_sb", tag="sin_sb")
-        sinx = const.tile([P, 32, 64], BF16, name="sinx", tag="sinx")
+        sinx_sb = const.tile([P, 32, 64], BF16, name="sinx_sb", tag="sinx_sb")
         ident = const.tile([P, P], F32, name="ident", tag="ident")
         x_sb = [xpool.tile([P, TILES, HIDDEN], BF16, name="x%d" % r, tag="x") for r in range(ROUNDS)]
 
         make_identity(nc, ident[:])
 
-        wqa_v = Wqa.rearrange("(u p e) k -> p u (e k)", u=2, p=P, e=2)
-        for u in range(2):
-            nc.sync.dma_start(
-                out=wqa_raw[:, 2 * u : 2 * u + 2, :].rearrange("p e k -> p (e k)"), in_=wqa_v[:, u, :]
-            )
-        for h in range(2):
-            nc.sync.dma_start(
-                out=x_sb[0][:, 2 * h : 2 * h + 2, :].rearrange("p i k -> p (i k)"),
-                in_=xv[:, 0, 2 * h * HIDDEN : (2 * h + 2) * HIDDEN],
-            )
-        nc.sync.dma_start(out=wkv_raw[:], in_=Wkva.rearrange("(b p) k -> p b k", p=P))
-        nc.sync.dma_start(out=wqb_raw[:, 0:2, :], in_=Wqb.rearrange("(h r) k -> r h k", h=2)[0:128, :, :])
-        nc.sync.dma_start(out=wqb_raw[0:64, 2, :], in_=Wqb[128:192, :])
-        nc.sync.dma_start(out=wqb_raw[64:128, 2, :], in_=Wqb[320:384, :])
-        nc.sync.dma_start(out=x_sb[1][:].rearrange("p i k -> p (i k)"), in_=xv[:, 1, :])
-        nc.sync.dma_start(out=cos_sb[:].rearrange("p t c -> p (t c)"), in_=cosv)
-        nc.sync.dma_start(out=sin_sb[:].rearrange("p t c -> p (t c)"), in_=sinv)
-        for r in range(2, ROUNDS):
-            nc.sync.dma_start(out=x_sb[r][:].rearrange("p i k -> p (i k)"), in_=xv[:, r, :])
+        def load(what):
+            if what in ("wqa0", "wqa1"):
+                u = 0 if what == "wqa0" else 1
+                nc.sync.dma_start(
+                    out=wqa_raw[:, 2 * u : 2 * u + 2, :].rearrange("p e k -> p (e k)"), in_=wqa_v[:, u, :]
+                )
+            elif what in ("x0p0", "x0p1"):
+                h = 0 if what == "x0p0" else 1
+                nc.sync.dma_start(
+                    out=x_sb[0][:, 2 * h : 2 * h + 2, :].rearrange("p i k -> p (i k)"),
+                    in_=xv[:, 0, 2 * h * HIDDEN : (2 * h + 2) * HIDDEN],
+                )
+            elif what == "wkv":
+                nc.sync.dma_start(out=wkv_raw[:], in_=Wkva.rearrange("(b p) k -> p b k", p=P))
+            elif what == "wqb":
+                nc.sync.dma_start(out=wqb_raw[:, 0:2, :], in_=Wqb.rearrange("(h r) k -> r h k", h=2)[0:128, :, :])
+                nc.sync.dma_start(out=wqb_raw[0:64, 2, :], in_=Wqb[128:192, :])
+                nc.sync.dma_start(out=wqb_raw[64:128, 2, :], in_=Wqb[320:384, :])
+            elif what == "cos":
+                nc.sync.dma_start(out=cos_sb[:].rearrange("p t c -> p (t c)"), in_=cosv)
+            elif what == "sin":
+                nc.sync.dma_start(out=sin_sb[:].rearrange("p t c -> p (t c)"), in_=sinv)
+            else:
+                r = int(what[1:])
+                nc.sync.dma_start(out=x_sb[r][:].rearrange("p i k -> p (i k)"), in_=xv[:, r, :])
 
         def new_bank(nm):
             return psum.tile([P, 512], F32, name=nm, tag="bank")
@@ -92,9 +96,9 @@ def tile_mlaselfattn_t_kernel(tc, x, cos, sin, Wqa, Wqb, Wkva, out):
                     )
             return bank[:, 0 : 2 * n].rearrange("p (u n) -> p n u", u=2)
 
-        def drain_words(eng_is_scalar, grouped2d, src):
+        def drain_words(on_scalar, grouped2d, src):
             dst = grouped2d.bitcast(F32).rearrange("p (n u) -> p n u", u=2)
-            if eng_is_scalar:
+            if on_scalar:
                 nc.scalar.copy(out=dst, in_=src)
             else:
                 nc.vector.tensor_copy(out=dst, in_=src)
@@ -108,9 +112,9 @@ def tile_mlaselfattn_t_kernel(tc, x, cos, sin, Wqa, Wqb, Wkva, out):
                 start=start, stop=stop,
             )
 
-        wqa_g = const.tile([P, 2, 512, 4], BF16, name="wqa_g", tag="wqa_g", align_bytes=64)
-        wqa_c = const.tile([P, 2, 512], U32, name="wqa_c", tag="wqa_c", align_bytes=64)
-        wqa_s = const.tile([P, 2, 512], U8, name="wqa_s", tag="wqa_s", align_bytes=64)
+        wqa_g = const.tile([P, 2, 2, 256, 4], BF16, name="wqa_g", tag="wqa_g", align_bytes=64)
+        wqa_c = const.tile([P, 2, 2, 256], U32, name="wqa_c", tag="wqa_c", align_bytes=64)
+        wqa_s = const.tile([P, 2, 2, 256], U8, name="wqa_s", tag="wqa_s", align_bytes=64)
         wkv_g = const.tile([P, 2, 256, 4], BF16, name="wkv_g", tag="wkv_g", align_bytes=64)
         wkv_c = const.tile([P, 2, 256], U32, name="wkv_c", tag="wkv_c", align_bytes=64)
         wkv_s = const.tile([P, 2, 256], U8, name="wkv_s", tag="wkv_s", align_bytes=64)
@@ -119,14 +123,15 @@ def tile_mlaselfattn_t_kernel(tc, x, cos, sin, Wqa, Wqb, Wkva, out):
         wqb_s = const.tile([P, 384], U8, name="wqb_s", tag="wqb_s", align_bytes=64)
 
         def prep_wqa():
-            k = 0
             for jp in range(2):
                 for g in range(2):
                     src = transpose_bank("wa%d%d" % (jp, g), [wqa_raw[:, 2 * jp, :], wqa_raw[:, 2 * jp + 1, :]], g)
-                    drain_words(k % 2 == 0, wqa_g[:, g, 256 * jp : 256 * jp + 256, :].rearrange("p n t -> p (n t)"), src)
-                    k += 1
-            for g in range(2):
-                quant(wqa_c[:, g, :], wqa_s[:, g, :], wqa_g[:, g, :, :].rearrange("p n t -> p (n t)"))
+                    drain_words(g == 0, wqa_g[:, jp, g, :, :].rearrange("p n t -> p (n t)"), src)
+                quant(
+                    wqa_c[:, jp, :, :].rearrange("p g n -> p (g n)"),
+                    wqa_s[:, jp, :, :].rearrange("p g n -> p (g n)"),
+                    wqa_g[:, jp, :, :, :].rearrange("p g n t -> p (g n t)"),
+                )
 
         def prep_wkv():
             for g in range(2):
@@ -146,8 +151,16 @@ def tile_mlaselfattn_t_kernel(tc, x, cos, sin, Wqa, Wqb, Wkva, out):
             quant(wqb_c[:, 0:256], wqb_s[:, 0:256], wqb_g[:, 0:256, :].rearrange("p n t -> p (n t)"))
             quant(wqb_c[:, 256:384], wqb_s[:, 256:384], wqb_g[:, 256:384, :].rearrange("p n t -> p (n t)"))
 
+        def sinx():
+            nc.vector.tensor_copy(out=sinx_sb[:, :, 0:32], in_=sin_sb[:, :, 32:64])
+            nc.vector.tensor_copy(out=sinx_sb[:, :, 32:64], in_=sin_sb[:, :, 0:32])
+
+        xg = {}
+        xsrc = {}
         xc = {}
         xs = {}
+        qbank = {}
+        qg = {}
         qc = {}
         qs = {}
         kbank = {}
@@ -155,48 +168,60 @@ def tile_mlaselfattn_t_kernel(tc, x, cos, sin, Wqa, Wqb, Wkva, out):
         pbank = {}
         osb = {}
         tk = {}
+        tq = {}
 
-        def stage_x(r, both_engines):
-            grouped = []
-            for pr in range(2):
-                xg = xgp.tile([P, 2, 256, 4], BF16, name="xg%d_%d" % (r, pr), tag="xg", align_bytes=64)
-                grouped.append(xg)
-                for g in range(2):
-                    src = transpose_bank(
-                        "xt%d_%d%d" % (r, pr, g), [x_sb[r][:, 2 * pr, :], x_sb[r][:, 2 * pr + 1, :]], g
-                    )
-                    drain_words((not both_engines) or g == 0, xg[:, g, :, :].rearrange("p n t -> p (n t)"), src)
-            for pr in range(2):
-                xc[(r, pr)] = xcp.tile([P, 2, 256], U32, name="xc%d_%d" % (r, pr), tag="xc", align_bytes=64)
-                xs[(r, pr)] = xcp.tile([P, 2, 256], U8, name="xs%d_%d" % (r, pr), tag="xs", align_bytes=64)
-                quant(
-                    xc[(r, pr)][:].rearrange("p g n -> p (g n)"),
-                    xs[(r, pr)][:].rearrange("p g n -> p (g n)"),
-                    grouped[pr][:].rearrange("p g n t -> p (g n t)"),
-                )
+        def xdst(r, pr, g):
+            return xg[(r, pr)][:, g, :, :].rearrange("p n t -> p (n t)")
 
-        def stage_qa(r, i):
+        def txb(r, pr, g, eng):
+            if (r, pr) not in xg:
+                xg[(r, pr)] = xgp.tile([P, 2, 256, 4], BF16, name="xg%d_%d" % (r, pr), tag="xg", align_bytes=64)
+            xsrc[(r, pr, g)] = transpose_bank(
+                "xt%d_%d%d" % (r, pr, g), [x_sb[r][:, 2 * pr, :], x_sb[r][:, 2 * pr + 1, :]], g
+            )
+            if eng == "S":
+                drain_words(True, xdst(r, pr, g), xsrc[(r, pr, g)])
+
+        def sx(r, pr, g):
+            drain_words(True, xdst(r, pr, g), xsrc[(r, pr, g)])
+
+        def vx(r, pr, g):
+            drain_words(False, xdst(r, pr, g), xsrc[(r, pr, g)])
+
+        def vqx(r, pr):
+            xc[(r, pr)] = xcp.tile([P, 2, 256], U32, name="xc%d_%d" % (r, pr), tag="xc", align_bytes=64)
+            xs[(r, pr)] = xcp.tile([P, 2, 256], U8, name="xs%d_%d" % (r, pr), tag="xs", align_bytes=64)
+            quant(
+                xc[(r, pr)][:].rearrange("p g n -> p (g n)"),
+                xs[(r, pr)][:].rearrange("p g n -> p (g n)"),
+                xg[(r, pr)][:].rearrange("p g n t -> p (g n t)"),
+            )
+
+        def a(r, i):
             pr, i2 = i // 2, i % 2
             cols = slice(i2 * P, (i2 + 1) * P)
             bank = new_bank("qa%d_%d" % (r, i))
+            qbank[(r, i)] = bank
             for j in range(4):
+                wc = slice((j % 2) * P, (j % 2 + 1) * P)
                 for g in range(2):
                     mx(
                         bank[:, j * P : (j + 1) * P],
-                        wqa_c[:, g, j * P : (j + 1) * P], wqa_s[:, g, j * P : (j + 1) * P],
+                        wqa_c[:, j // 2, g, wc], wqa_s[:, j // 2, g, wc],
                         xc[(r, pr)][:, g, cols], xs[(r, pr)][:, g, cols],
                         g == 0, g == 1,
                     )
-            qg = qgp.tile([P, P, 4], BF16, name="qg%d_%d" % (r, i), tag="qg", align_bytes=64)
-            nc.scalar.copy(out=qg[:], in_=bank[:].rearrange("p (j n) -> p n j", j=4))
-            return qg
 
-        def quant_qa(r, i, qg):
+        def sa(r, i):
+            qg[(r, i)] = qgp.tile([P, P, 4], BF16, name="qg%d_%d" % (r, i), tag="qg", align_bytes=64)
+            nc.scalar.copy(out=qg[(r, i)][:], in_=qbank[(r, i)][:].rearrange("p (j n) -> p n j", j=4))
+
+        def vqa(r, i):
             qc[(r, i)] = qcp.tile([P, P], U32, name="qc%d_%d" % (r, i), tag="qc", align_bytes=64)
             qs[(r, i)] = qcp.tile([P, P], U8, name="qs%d_%d" % (r, i), tag="qs", align_bytes=64)
-            quant(qc[(r, i)][:], qs[(r, i)][:], qg[:].rearrange("p n t -> p (n t)"))
+            quant(qc[(r, i)][:], qs[(r, i)][:], qg[(r, i)][:].rearrange("p n t -> p (n t)"))
 
-        def pe_kv(r, pr):
+        def k(r, pr):
             bank = new_bank("kv%d_%d" % (r, pr))
             kbank[(r, pr)] = bank
             for i2 in range(2):
@@ -209,84 +234,341 @@ def tile_mlaselfattn_t_kernel(tc, x, cos, sin, Wqa, Wqb, Wkva, out):
                         g == 0, g == 1,
                     )
 
-        def pe_q(r):
-            pbank[r] = None
+        def q_pass(r, i, nb, ncol, pb, pcol):
+            mx(nb[:, ncol : ncol + 256], qc[(r, i)][:], qs[(r, i)][:], wqb_c[:, 0:256], wqb_s[:, 0:256], True, True)
+            mx(pb[:, pcol : pcol + P], qc[(r, i)][:], qs[(r, i)][:], wqb_c[:, 256:384], wqb_s[:, 256:384], True, True)
+
+        def q(r):
             for pr in range(2):
                 nbank[(r, pr)] = new_bank("qn%d_%d" % (r, pr))
                 if pr == 0:
-                    pbank[r] = new_bank("qp%d" % r)
+                    pbank[(r, 0)] = new_bank("qp%d" % r)
                 for i2 in range(2):
                     i = 2 * pr + i2
-                    mx(
-                        nbank[(r, pr)][:, i2 * 256 : (i2 + 1) * 256],
-                        qc[(r, i)][:], qs[(r, i)][:], wqb_c[:, 0:256], wqb_s[:, 0:256], True, True,
-                    )
-                    mx(
-                        pbank[r][:, i * P : (i + 1) * P],
-                        qc[(r, i)][:], qs[(r, i)][:], wqb_c[:, 256:384], wqb_s[:, 256:384], True, True,
-                    )
+                    q_pass(r, i, nbank[(r, pr)], i2 * 256, pbank[(r, 0)], i * P)
 
-        def v_kv(r, pr):
+        def qpair(r, pr):
+            nbank[(r, pr)] = new_bank("qn%d_%d" % (r, pr))
+            pbank[(r, 2 * pr)] = new_bank("qp%d_%d" % (r, pr))
+            for i2 in range(2):
+                q_pass(r, 2 * pr + i2, nbank[(r, pr)], i2 * 256, pbank[(r, 2 * pr)], i2 * P)
+
+        def get_o(r):
+            if r not in osb:
+                osb[r] = outp.tile([P, TILES, OUT_W], F32, name="o%d" % r, tag="o")
+            return osb[r]
+
+        def vk(r, pr):
+            if r not in tk:
+                tk[r] = tmpp.tile([P, TILES, 64], F32, name="tk%d" % r, tag="tk")
             kv = kbank[(r, pr)][:].rearrange("p (i c) -> p i c", i=2)
-            o = osb[r]
+            o = get_o(r)
             t0 = TILES * r + 2 * pr
             rows = slice(2 * pr, 2 * pr + 2)
             nc.vector.tensor_tensor(out=o[:, rows, 384:448], in0=kv[:, :, 192:256], in1=cos_sb[:, t0 : t0 + 2, :], op=MULT)
-            nc.vector.tensor_tensor(out=tk[r][:, rows, :], in0=kv[:, :, 192:256], in1=sinx[:, t0 : t0 + 2, :], op=MULT)
+            nc.vector.tensor_tensor(out=tk[r][:, rows, :], in0=kv[:, :, 192:256], in1=sinx_sb[:, t0 : t0 + 2, :], op=MULT)
             nc.vector.tensor_copy(out=o[:, rows, 448:640], in_=kv[:, :, 0:192])
 
-        def s_nope(r, pr):
-            o = osb[r][:, 2 * pr : 2 * pr + 2, 0:384].rearrange("p i (h c) -> p i h c", h=2)
+        def sn(r, pr):
+            o = get_o(r)[:, 2 * pr : 2 * pr + 2, 0:384].rearrange("p i (h c) -> p i h c", h=2)
             nc.scalar.copy(out=o[:, :, :, 0:128], in_=nbank[(r, pr)][:].rearrange("p (i h c) -> p i h c", i=2, h=2))
 
-        def v_rope(r):
-            o = osb[r]
-            oq = o[:, :, 0:384].rearrange("p i (h c) -> p i h c", h=2)
-            pe = pbank[r][:].rearrange("p (i h c) -> p i h c", i=4, h=2)
-            t0 = TILES * r
-            cb = cos_sb[:, t0 : t0 + 4, :].unsqueeze(2).to_broadcast([P, 4, 2, 64])
-            sb = sinx[:, t0 : t0 + 4, :].unsqueeze(2).to_broadcast([P, 4, 2, 64])
-            tq = tmpp.tile([P, 4, 2, 64], F32, name="tq%d" % r, tag="tq")
+        def ab(r, i0, n):
+            if r not in tq:
+                tq[r] = tmpp.tile([P, TILES, 2, 64], F32, name="tq%d" % r, tag="tq")
+            oq = get_o(r)[:, i0 : i0 + n, 0:384].rearrange("p i (h c) -> p i h c", h=2)
+            pe = pbank[(r, i0)][:, 0 : n * P].rearrange("p (i h c) -> p i h c", i=n, h=2)
+            t0 = TILES * r + i0
+            cb = cos_sb[:, t0 : t0 + n, :].unsqueeze(2).to_broadcast([P, n, 2, 64])
+            sb = sinx_sb[:, t0 : t0 + n, :].unsqueeze(2).to_broadcast([P, n, 2, 64])
             nc.vector.tensor_tensor(out=oq[:, :, :, 128:192], in0=pe, in1=cb, op=MULT)
-            nc.vector.tensor_tensor(out=tq[:], in0=pe, in1=sb, op=MULT)
-            nc.vector.tensor_tensor(out=o[:, :, 384:416], in0=o[:, :, 384:416], in1=tk[r][:, :, 32:64], op=SUB)
-            nc.vector.tensor_tensor(out=o[:, :, 416:448], in0=o[:, :, 416:448], in1=tk[r][:, :, 0:32], op=ADD)
-            nc.vector.tensor_tensor(out=oq[:, :, :, 128:160], in0=oq[:, :, :, 128:160], in1=tq[:, :, :, 32:64], op=SUB)
-            nc.vector.tensor_tensor(out=oq[:, :, :, 160:192], in0=oq[:, :, :, 160:192], in1=tq[:, :, :, 0:32], op=ADD)
+            nc.vector.tensor_tensor(out=tq[r][:, i0 : i0 + n, :, :], in0=pe, in1=sb, op=MULT)
 
-        def store(r):
-            nc.sync.dma_start(out=ov[:, r, :], in_=osb[r][:].rearrange("p i c -> p (i c)"))
+        def engine(e):
+            return nc.gpsimd if e == "G" else nc.vector
 
+        def ck_rows(r, rows, e):
+            o = osb[r]
+            engine(e).tensor_tensor(out=o[:, rows, 384:416], in0=o[:, rows, 384:416], in1=tk[r][:, rows, 32:64], op=SUB)
+            engine(e).tensor_tensor(out=o[:, rows, 416:448], in0=o[:, rows, 416:448], in1=tk[r][:, rows, 0:32], op=ADD)
+
+        def ck(r, e):
+            ck_rows(r, slice(0, TILES), e)
+
+        def ckp(r, pr, e):
+            ck_rows(r, slice(2 * pr, 2 * pr + 2), e)
+
+        def cq(r, i0, n, e):
+            oq = osb[r][:, i0 : i0 + n, 0:384].rearrange("p i (h c) -> p i h c", h=2)
+            t = tq[r][:, i0 : i0 + n, :, :]
+            engine(e).tensor_tensor(out=oq[:, :, :, 128:160], in0=oq[:, :, :, 128:160], in1=t[:, :, :, 32:64], op=SUB)
+            engine(e).tensor_tensor(out=oq[:, :, :, 160:192], in0=oq[:, :, :, 160:192], in1=t[:, :, :, 0:32], op=ADD)
+
+        def store(r, prs, parts):
+            i0 = 2 * prs[0]
+            n = 2 * len(prs)
+            c0 = 0 if "q" in parts else 384
+            c1 = OUT_W if "kv" in parts else 384
+            nc.sync.dma_start(out=ov[:, r, i0 : i0 + n, c0:c1], in_=osb[r][:, i0 : i0 + n, c0:c1])
+
+        load("wqa0")
+        load("wqa1")
+        load("x0p0")
+        load("x0p1")
+        load("wkv")
+        load("wqb")
+        load("x1")
+        load("cos")
+        load("sin")
+        load("x2")
+        load("x3")
+        load("x4")
+        load("x5")
+        load("x6")
+        load("x7")
         prep_wqa()
-        stage_x(0, True)
-        for r in range(ROUNDS):
-            qg0 = stage_qa(r, 0)
-            qg1 = stage_qa(r, 1)
-            if r > 0:
-                v_rope(r - 1)
-                store(r - 1)
-            quant_qa(r, 0, qg0)
-            quant_qa(r, 1, qg1)
-            if r == 0:
-                prep_wkv()
-                prep_wqb()
-            if r + 1 < ROUNDS:
-                stage_x(r + 1, r == 0)
-            qg2 = stage_qa(r, 2)
-            quant_qa(r, 2, qg2)
-            qg3 = stage_qa(r, 3)
-            quant_qa(r, 3, qg3)
-            pe_kv(r, 0)
-            pe_kv(r, 1)
-            pe_q(r)
-            osb[r] = outp.tile([P, TILES, OUT_W], F32, name="o%d" % r, tag="o")
-            tk[r] = tmpp.tile([P, TILES, 64], F32, name="tk%d" % r, tag="tk")
-            if r == 0:
-                nc.vector.tensor_copy(out=sinx[:, :, 0:32], in_=sin_sb[:, :, 32:64])
-                nc.vector.tensor_copy(out=sinx[:, :, 32:64], in_=sin_sb[:, :, 0:32])
-            v_kv(r, 0)
-            v_kv(r, 1)
-            s_nope(r, 0)
-            s_nope(r, 1)
-        v_rope(ROUNDS - 1)
-        store(ROUNDS - 1)
+        txb(0, 0, 0, "S")
+        txb(0, 0, 1, "later")
+        txb(0, 1, 0, "S")
+        txb(0, 1, 1, "later")
+        vx(0, 0, 1)
+        vqx(0, 0)
+        vx(0, 1, 1)
+        vqx(0, 1)
+        prep_wkv()
+        a(0, 0)
+        sa(0, 0)
+        vqa(0, 0)
+        a(0, 1)
+        sa(0, 1)
+        vqa(0, 1)
+        a(0, 2)
+        sa(0, 2)
+        vqa(0, 2)
+        a(0, 3)
+        sa(0, 3)
+        vqa(0, 3)
+        prep_wqb()
+        txb(1, 0, 0, "S")
+        txb(1, 0, 1, "later")
+        txb(1, 1, 0, "S")
+        txb(1, 1, 1, "later")
+        vx(1, 0, 1)
+        vqx(1, 0)
+        vx(1, 1, 1)
+        vqx(1, 1)
+        sinx()
+        k(0, 0)
+        k(0, 1)
+        vk(0, 0)
+        vk(0, 1)
+        txb(2, 0, 0, "S")
+        txb(2, 0, 1, "S")
+        txb(2, 1, 0, "S")
+        txb(2, 1, 1, "S")
+        q(0)
+        sn(0, 0)
+        sn(0, 1)
+        k(1, 0)
+        k(1, 1)
+        ab(0, 0, 4)
+        ck(0, "V")
+        cq(0, 0, 4, "V")
+        store(0, [0, 1], ["q", "kv"])
+        a(1, 0)
+        sa(1, 0)
+        vk(1, 0)
+        vqa(1, 0)
+        a(1, 1)
+        sa(1, 1)
+        vk(1, 1)
+        vqa(1, 1)
+        a(1, 2)
+        sa(1, 2)
+        vqa(1, 2)
+        vqx(2, 0)
+        a(1, 3)
+        sa(1, 3)
+        vqa(1, 3)
+        vqx(2, 1)
+        txb(3, 0, 0, "S")
+        txb(3, 0, 1, "S")
+        txb(3, 1, 0, "S")
+        txb(3, 1, 1, "S")
+        q(1)
+        sn(1, 0)
+        sn(1, 1)
+        k(2, 0)
+        k(2, 1)
+        ab(1, 0, 4)
+        ck(1, "V")
+        cq(1, 0, 4, "V")
+        store(1, [0, 1], ["q", "kv"])
+        a(2, 0)
+        sa(2, 0)
+        vk(2, 0)
+        vqa(2, 0)
+        a(2, 1)
+        sa(2, 1)
+        vk(2, 1)
+        vqa(2, 1)
+        a(2, 2)
+        sa(2, 2)
+        vqa(2, 2)
+        vqx(3, 0)
+        a(2, 3)
+        sa(2, 3)
+        vqa(2, 3)
+        vqx(3, 1)
+        txb(4, 0, 0, "S")
+        txb(4, 0, 1, "S")
+        txb(4, 1, 0, "S")
+        txb(4, 1, 1, "S")
+        q(2)
+        sn(2, 0)
+        sn(2, 1)
+        k(3, 0)
+        k(3, 1)
+        ab(2, 0, 4)
+        ck(2, "V")
+        cq(2, 0, 4, "V")
+        store(2, [0, 1], ["q", "kv"])
+        a(3, 0)
+        sa(3, 0)
+        vk(3, 0)
+        vqa(3, 0)
+        a(3, 1)
+        sa(3, 1)
+        vk(3, 1)
+        vqa(3, 1)
+        a(3, 2)
+        sa(3, 2)
+        vqa(3, 2)
+        vqx(4, 0)
+        a(3, 3)
+        sa(3, 3)
+        vqa(3, 3)
+        vqx(4, 1)
+        txb(5, 0, 0, "S")
+        txb(5, 0, 1, "S")
+        txb(5, 1, 0, "S")
+        txb(5, 1, 1, "S")
+        q(3)
+        sn(3, 0)
+        sn(3, 1)
+        k(4, 0)
+        k(4, 1)
+        ab(3, 0, 4)
+        ck(3, "V")
+        cq(3, 0, 4, "V")
+        store(3, [0, 1], ["q", "kv"])
+        a(4, 0)
+        sa(4, 0)
+        vk(4, 0)
+        vqa(4, 0)
+        a(4, 1)
+        sa(4, 1)
+        vk(4, 1)
+        vqa(4, 1)
+        a(4, 2)
+        sa(4, 2)
+        vqa(4, 2)
+        vqx(5, 0)
+        a(4, 3)
+        sa(4, 3)
+        vqa(4, 3)
+        vqx(5, 1)
+        txb(6, 0, 0, "S")
+        txb(6, 0, 1, "S")
+        txb(6, 1, 0, "S")
+        txb(6, 1, 1, "S")
+        q(4)
+        sn(4, 0)
+        sn(4, 1)
+        k(5, 0)
+        k(5, 1)
+        ab(4, 0, 4)
+        ck(4, "V")
+        cq(4, 0, 4, "V")
+        store(4, [0, 1], ["q", "kv"])
+        a(5, 0)
+        sa(5, 0)
+        vk(5, 0)
+        vqa(5, 0)
+        a(5, 1)
+        sa(5, 1)
+        vk(5, 1)
+        vqa(5, 1)
+        a(5, 2)
+        sa(5, 2)
+        vqa(5, 2)
+        vqx(6, 0)
+        a(5, 3)
+        sa(5, 3)
+        vqa(5, 3)
+        vqx(6, 1)
+        txb(7, 0, 0, "S")
+        txb(7, 0, 1, "S")
+        txb(7, 1, 0, "S")
+        txb(7, 1, 1, "S")
+        q(5)
+        sn(5, 0)
+        sn(5, 1)
+        k(6, 0)
+        k(6, 1)
+        ab(5, 0, 4)
+        ck(5, "G")
+        vqx(7, 0)
+        cq(5, 0, 4, "V")
+        store(5, [0, 1], ["q", "kv"])
+        a(6, 0)
+        sa(6, 0)
+        vk(6, 0)
+        vqa(6, 0)
+        a(6, 1)
+        sa(6, 1)
+        vk(6, 1)
+        vqa(6, 1)
+        a(6, 2)
+        sa(6, 2)
+        vqa(6, 2)
+        a(6, 3)
+        sa(6, 3)
+        vqa(6, 3)
+        a(7, 0)
+        sa(7, 0)
+        a(7, 1)
+        sa(7, 1)
+        vqx(7, 1)
+        q(6)
+        sn(6, 0)
+        sn(6, 1)
+        ck(6, "V")
+        a(7, 2)
+        sa(7, 2)
+        k(7, 0)
+        a(7, 3)
+        sa(7, 3)
+        ab(6, 0, 4)
+        cq(6, 0, 4, "V")
+        vqa(7, 0)
+        vqa(7, 1)
+        vqa(7, 2)
+        vk(7, 0)
+        vqa(7, 3)
+        store(6, [0, 1], ["q", "kv"])
+        k(7, 1)
+        qpair(7, 0)
+        qpair(7, 1)
+        ckp(7, 0, "G")
+        sn(7, 0)
+        ab(7, 0, 2)
+        cq(7, 0, 2, "V")
+        store(7, [0], ["q", "kv"])
+        vk(7, 1)
+        ab(7, 2, 2)
+        ckp(7, 1, "G")
+        sn(7, 1)
+        cq(7, 2, 2, "V")
+        store(7, [1], ["kv"])
+        store(7, [1], ["q"])

@@ -41,7 +41,7 @@ def tile_mlaselfattn_t_kernel(tc, x, cos, sin, Wqa, Wqb, Wkva, out):
         ov = out.flatten_outer_dims().rearrange("(p r i) c -> p r i c", p=P, r=ROUNDS, i=TILES)
         cosv = cos.flatten_outer_dims().rearrange("(p t) c -> p (t c)", p=P)
         sinv = sin.flatten_outer_dims().rearrange("(p t) c -> p (t c)", p=P)
-        wqa_v = Wqa.rearrange("(u p e) k -> p u (e k)", u=2, p=P, e=2)
+        wqa_v = Wqa.rearrange("(u p e) k -> p u e k", u=2, p=P, e=2)
 
         wqa_raw = const.tile([P, 4, HIDDEN], BF16, name="wqa_raw", tag="wqa_raw")
         wkv_raw = const.tile([P, 2, HIDDEN], BF16, name="wkv_raw", tag="wkv_raw")
@@ -55,17 +55,12 @@ def tile_mlaselfattn_t_kernel(tc, x, cos, sin, Wqa, Wqb, Wkva, out):
         make_identity(nc, ident[:])
 
         def load(what):
-            if what in ("wqa0", "wqa1"):
-                u = 0 if what == "wqa0" else 1
-                nc.sync.dma_start(
-                    out=wqa_raw[:, 2 * u : 2 * u + 2, :].rearrange("p e k -> p (e k)"), in_=wqa_v[:, u, :]
-                )
-            elif what in ("x0p0", "x0p1"):
-                h = 0 if what == "x0p0" else 1
-                nc.sync.dma_start(
-                    out=x_sb[0][:, 2 * h : 2 * h + 2, :].rearrange("p i k -> p (i k)"),
-                    in_=xv[:, 0, 2 * h * HIDDEN : (2 * h + 2) * HIDDEN],
-                )
+            if what[0:3] == "wqa":
+                j = int(what[3:])
+                nc.sync.dma_start(out=wqa_raw[:, j, :], in_=wqa_v[:, j // 2, j % 2, :])
+            elif what[0:3] == "x0t":
+                i = int(what[3:])
+                nc.sync.dma_start(out=x_sb[0][:, i, :], in_=xv[:, 0, i * HIDDEN : (i + 1) * HIDDEN])
             elif what == "wkv":
                 nc.sync.dma_start(out=wkv_raw[:], in_=Wkva.rearrange("(b p) k -> p b k", p=P))
             elif what == "wqb":
@@ -96,12 +91,25 @@ def tile_mlaselfattn_t_kernel(tc, x, cos, sin, Wqa, Wqb, Wkva, out):
                     )
             return bank[:, 0 : 2 * n].rearrange("p (u n) -> p n u", u=2)
 
-        def drain_words(on_scalar, grouped2d, src):
-            dst = grouped2d.bitcast(F32).rearrange("p (n u) -> p n u", u=2)
-            if on_scalar:
+        def copy_out(eng, dst, src):
+            if eng == "S":
                 nc.scalar.copy(out=dst, in_=src)
             else:
                 nc.vector.tensor_copy(out=dst, in_=src)
+
+        def drain_words(eng, grouped2d, src):
+            copy_out(eng, grouped2d.bitcast(F32).rearrange("p (n u) -> p n u", u=2), src)
+
+        def transpose_rows(nm, block):
+            bank = new_bank(nm)
+            for w in range(4):
+                nc.tensor.transpose(
+                    out=bank[:, w * P : (w + 1) * P], in_=block.bitcast(F32)[:, w * P : (w + 1) * P], identity=ident[:]
+                )
+            return bank[:].rearrange("p (g u n) -> p g n u", g=2, u=2)
+
+        def drain_rows(eng, grouped2d, src):
+            copy_out(eng, grouped2d.bitcast(F32).rearrange("p (g n u) -> p g n u", g=2, u=2), src)
 
         def quant(codes, scales, grouped2d):
             nc.vector.quantize_mx(out=codes.bitcast(FP8X4), scales=scales, in_=grouped2d)
@@ -112,9 +120,9 @@ def tile_mlaselfattn_t_kernel(tc, x, cos, sin, Wqa, Wqb, Wkva, out):
                 start=start, stop=stop,
             )
 
-        wqa_g = const.tile([P, 2, 2, 256, 4], BF16, name="wqa_g", tag="wqa_g", align_bytes=64)
-        wqa_c = const.tile([P, 2, 2, 256], U32, name="wqa_c", tag="wqa_c", align_bytes=64)
-        wqa_s = const.tile([P, 2, 2, 256], U8, name="wqa_s", tag="wqa_s", align_bytes=64)
+        wqa_g = const.tile([P, 4, 2, P, 4], BF16, name="wqa_g", tag="wqa_g", align_bytes=64)
+        wqa_c = const.tile([P, 4, 2, P], U32, name="wqa_c", tag="wqa_c", align_bytes=64)
+        wqa_s = const.tile([P, 4, 2, P], U8, name="wqa_s", tag="wqa_s", align_bytes=64)
         wkv_g = const.tile([P, 2, 256, 4], BF16, name="wkv_g", tag="wkv_g", align_bytes=64)
         wkv_c = const.tile([P, 2, 256], U32, name="wkv_c", tag="wkv_c", align_bytes=64)
         wkv_s = const.tile([P, 2, 256], U8, name="wkv_s", tag="wkv_s", align_bytes=64)
@@ -122,34 +130,39 @@ def tile_mlaselfattn_t_kernel(tc, x, cos, sin, Wqa, Wqb, Wkva, out):
         wqb_c = const.tile([P, 384], U32, name="wqb_c", tag="wqb_c", align_bytes=64)
         wqb_s = const.tile([P, 384], U8, name="wqb_s", tag="wqb_s", align_bytes=64)
 
-        def prep_wqa():
-            for jp in range(2):
-                for g in range(2):
-                    src = transpose_bank("wa%d%d" % (jp, g), [wqa_raw[:, 2 * jp, :], wqa_raw[:, 2 * jp + 1, :]], g)
-                    drain_words(g == 0, wqa_g[:, jp, g, :, :].rearrange("p n t -> p (n t)"), src)
-                quant(
-                    wqa_c[:, jp, :, :].rearrange("p g n -> p (g n)"),
-                    wqa_s[:, jp, :, :].rearrange("p g n -> p (g n)"),
-                    wqa_g[:, jp, :, :, :].rearrange("p g n t -> p (g n t)"),
-                )
+        def wqa_t(j, eng):
+            src = transpose_rows("wa%d" % j, wqa_raw[:, j, :])
+            drain_rows(eng, wqa_g[:, j, :, :, :].rearrange("p g n t -> p (g n t)"), src)
 
-        def prep_wkv():
-            for g in range(2):
-                src = transpose_bank("wk%d" % g, [wkv_raw[:, 0, :], wkv_raw[:, 1, :]], g)
-                drain_words(g == 0, wkv_g[:, g, :, :].rearrange("p n t -> p (n t)"), src)
+        def wqa_q(j):
+            quant(
+                wqa_c[:, j, :, :].rearrange("p g n -> p (g n)"),
+                wqa_s[:, j, :, :].rearrange("p g n -> p (g n)"),
+                wqa_g[:, j, :, :, :].rearrange("p g n t -> p (g n t)"),
+            )
+
+        def wkv_t(g, eng):
+            src = transpose_bank("wk%d" % g, [wkv_raw[:, 0, :], wkv_raw[:, 1, :]], g)
+            drain_words(eng, wkv_g[:, g, :, :].rearrange("p n t -> p (n t)"), src)
+
+        def wkv_q():
             quant(
                 wkv_c[:].rearrange("p g n -> p (g n)"),
                 wkv_s[:].rearrange("p g n -> p (g n)"),
                 wkv_g[:].rearrange("p g n t -> p (g n t)"),
             )
 
-        def prep_wqb():
-            src = transpose_bank("wb0", [wqb_raw[:, 0, :], wqb_raw[:, 1, :]], 0)
-            drain_words(True, wqb_g[:, 0:256, :].rearrange("p n t -> p (n t)"), src)
-            src = transpose_bank("wb1", [wqb_raw[:, 2, :]], 0)
-            drain_words(False, wqb_g[:, 256:384, :].rearrange("p n t -> p (n t)"), src)
-            quant(wqb_c[:, 0:256], wqb_s[:, 0:256], wqb_g[:, 0:256, :].rearrange("p n t -> p (n t)"))
-            quant(wqb_c[:, 256:384], wqb_s[:, 256:384], wqb_g[:, 256:384, :].rearrange("p n t -> p (n t)"))
+        def wqb_t(b, eng):
+            if b == 0:
+                src = transpose_bank("wb0", [wqb_raw[:, 0, :], wqb_raw[:, 1, :]], 0)
+                drain_words(eng, wqb_g[:, 0:256, :].rearrange("p n t -> p (n t)"), src)
+            else:
+                src = transpose_bank("wb1", [wqb_raw[:, 2, :]], 0)
+                drain_words(eng, wqb_g[:, 256:384, :].rearrange("p n t -> p (n t)"), src)
+
+        def wqb_q(b):
+            c = slice(0, 256) if b == 0 else slice(256, 384)
+            quant(wqb_c[:, c], wqb_s[:, c], wqb_g[:, c, :].rearrange("p n t -> p (n t)"))
 
         def sinx():
             nc.vector.tensor_copy(out=sinx_sb[:, :, 0:32], in_=sin_sb[:, :, 32:64])
@@ -170,45 +183,50 @@ def tile_mlaselfattn_t_kernel(tc, x, cos, sin, Wqa, Wqb, Wkva, out):
         tk = {}
         tq = {}
 
-        def xdst(r, pr, g):
-            return xg[(r, pr)][:, g, :, :].rearrange("p n t -> p (n t)")
+        def xdst(r, i):
+            return xg[(r, i // 2)][:, i % 2, :, :, :].rearrange("p g n t -> p (g n t)")
 
-        def txb(r, pr, g, eng):
-            if (r, pr) not in xg:
-                xg[(r, pr)] = xgp.tile([P, 2, 256, 4], BF16, name="xg%d_%d" % (r, pr), tag="xg", align_bytes=64)
-            xsrc[(r, pr, g)] = transpose_bank(
-                "xt%d_%d%d" % (r, pr, g), [x_sb[r][:, 2 * pr, :], x_sb[r][:, 2 * pr + 1, :]], g
-            )
+        def tx(r, i, eng):
+            if (r, i // 2) not in xg:
+                xg[(r, i // 2)] = xgp.tile([P, 2, 2, P, 4], BF16, name="xg%d_%d" % (r, i // 2), tag="xg", align_bytes=64)
+            xsrc[(r, i)] = transpose_rows("xt%d_%d" % (r, i), x_sb[r][:, i, :])
             if eng == "S":
-                drain_words(True, xdst(r, pr, g), xsrc[(r, pr, g)])
+                drain_rows("S", xdst(r, i), xsrc[(r, i)])
 
-        def sx(r, pr, g):
-            drain_words(True, xdst(r, pr, g), xsrc[(r, pr, g)])
+        def vx(r, i):
+            drain_rows("V", xdst(r, i), xsrc[(r, i)])
 
-        def vx(r, pr, g):
-            drain_words(False, xdst(r, pr, g), xsrc[(r, pr, g)])
+        def new_codes(r, pr):
+            if (r, pr) not in xc:
+                xc[(r, pr)] = xcp.tile([P, 2, 2, P], U32, name="xc%d_%d" % (r, pr), tag="xc", align_bytes=64)
+                xs[(r, pr)] = xcp.tile([P, 2, 2, P], U8, name="xs%d_%d" % (r, pr), tag="xs", align_bytes=64)
 
         def vqx(r, pr):
-            xc[(r, pr)] = xcp.tile([P, 2, 256], U32, name="xc%d_%d" % (r, pr), tag="xc", align_bytes=64)
-            xs[(r, pr)] = xcp.tile([P, 2, 256], U8, name="xs%d_%d" % (r, pr), tag="xs", align_bytes=64)
+            new_codes(r, pr)
             quant(
-                xc[(r, pr)][:].rearrange("p g n -> p (g n)"),
-                xs[(r, pr)][:].rearrange("p g n -> p (g n)"),
-                xg[(r, pr)][:].rearrange("p g n t -> p (g n t)"),
+                xc[(r, pr)][:].rearrange("p i g n -> p (i g n)"),
+                xs[(r, pr)][:].rearrange("p i g n -> p (i g n)"),
+                xg[(r, pr)][:].rearrange("p i g n t -> p (i g n t)"),
+            )
+
+        def vqt(r, i):
+            new_codes(r, i // 2)
+            quant(
+                xc[(r, i // 2)][:, i % 2, :, :].rearrange("p g n -> p (g n)"),
+                xs[(r, i // 2)][:, i % 2, :, :].rearrange("p g n -> p (g n)"),
+                xdst(r, i),
             )
 
         def a(r, i):
             pr, i2 = i // 2, i % 2
-            cols = slice(i2 * P, (i2 + 1) * P)
             bank = new_bank("qa%d_%d" % (r, i))
             qbank[(r, i)] = bank
             for j in range(4):
-                wc = slice((j % 2) * P, (j % 2 + 1) * P)
                 for g in range(2):
                     mx(
                         bank[:, j * P : (j + 1) * P],
-                        wqa_c[:, j // 2, g, wc], wqa_s[:, j // 2, g, wc],
-                        xc[(r, pr)][:, g, cols], xs[(r, pr)][:, g, cols],
+                        wqa_c[:, j, g, :], wqa_s[:, j, g, :],
+                        xc[(r, pr)][:, i2, g, :], xs[(r, pr)][:, i2, g, :],
                         g == 0, g == 1,
                     )
 
@@ -225,11 +243,10 @@ def tile_mlaselfattn_t_kernel(tc, x, cos, sin, Wqa, Wqb, Wkva, out):
             bank = new_bank("kv%d_%d" % (r, pr))
             kbank[(r, pr)] = bank
             for i2 in range(2):
-                cols = slice(i2 * P, (i2 + 1) * P)
                 for g in range(2):
                     mx(
                         bank[:, i2 * 256 : (i2 + 1) * 256],
-                        xc[(r, pr)][:, g, cols], xs[(r, pr)][:, g, cols],
+                        xc[(r, pr)][:, i2, g, :], xs[(r, pr)][:, i2, g, :],
                         wkv_c[:, g, :], wkv_s[:, g, :],
                         g == 0, g == 1,
                     )
@@ -313,29 +330,41 @@ def tile_mlaselfattn_t_kernel(tc, x, cos, sin, Wqa, Wqb, Wkva, out):
 
         load("wqa0")
         load("wqa1")
-        load("x0p0")
-        load("x0p1")
+        load("wqa2")
+        load("wqa3")
+        load("x0t0")
+        load("x0t1")
+        load("x0t2")
+        load("x0t3")
         load("wkv")
         load("wqb")
+        load("sin")
         load("x1")
         load("cos")
-        load("sin")
         load("x2")
         load("x3")
         load("x4")
         load("x5")
         load("x6")
         load("x7")
-        prep_wqa()
-        txb(0, 0, 0, "S")
-        txb(0, 0, 1, "later")
-        txb(0, 1, 0, "S")
-        txb(0, 1, 1, "later")
-        vx(0, 0, 1)
-        vqx(0, 0)
-        vx(0, 1, 1)
-        vqx(0, 1)
-        prep_wkv()
+        wqa_t(0, "S")
+        wqa_q(0)
+        wqa_t(1, "V")
+        wqa_q(1)
+        wqa_t(2, "S")
+        wqa_q(2)
+        wqa_t(3, "V")
+        wqa_q(3)
+        tx(0, 0, "S")
+        vqt(0, 0)
+        tx(0, 1, "later")
+        vx(0, 1)
+        vqt(0, 1)
+        tx(0, 2, "S")
+        vqt(0, 2)
+        tx(0, 3, "later")
+        vx(0, 3)
+        vqt(0, 3)
         a(0, 0)
         sa(0, 0)
         vqa(0, 0)
@@ -345,27 +374,31 @@ def tile_mlaselfattn_t_kernel(tc, x, cos, sin, Wqa, Wqb, Wkva, out):
         a(0, 2)
         sa(0, 2)
         vqa(0, 2)
+        sinx()
         a(0, 3)
         sa(0, 3)
         vqa(0, 3)
-        prep_wqb()
-        txb(1, 0, 0, "S")
-        txb(1, 0, 1, "later")
-        txb(1, 1, 0, "S")
-        txb(1, 1, 1, "later")
-        vx(1, 0, 1)
-        vqx(1, 0)
-        vx(1, 1, 1)
-        vqx(1, 1)
-        sinx()
+        wkv_t(0, "S")
+        wkv_t(1, "V")
+        wkv_q()
+        wqb_t(0, "V")
+        wqb_t(1, "V")
+        wqb_q(0)
+        wqb_q(1)
+        tx(1, 0, "S")
+        tx(1, 1, "S")
+        tx(1, 2, "S")
+        tx(1, 3, "S")
         k(0, 0)
         k(0, 1)
         vk(0, 0)
+        vqx(1, 0)
         vk(0, 1)
-        txb(2, 0, 0, "S")
-        txb(2, 0, 1, "S")
-        txb(2, 1, 0, "S")
-        txb(2, 1, 1, "S")
+        vqx(1, 1)
+        tx(2, 0, "S")
+        tx(2, 1, "S")
+        tx(2, 2, "S")
+        tx(2, 3, "S")
         q(0)
         sn(0, 0)
         sn(0, 1)
@@ -391,10 +424,10 @@ def tile_mlaselfattn_t_kernel(tc, x, cos, sin, Wqa, Wqb, Wkva, out):
         sa(1, 3)
         vqa(1, 3)
         vqx(2, 1)
-        txb(3, 0, 0, "S")
-        txb(3, 0, 1, "S")
-        txb(3, 1, 0, "S")
-        txb(3, 1, 1, "S")
+        tx(3, 0, "S")
+        tx(3, 1, "S")
+        tx(3, 2, "S")
+        tx(3, 3, "S")
         q(1)
         sn(1, 0)
         sn(1, 1)
@@ -420,10 +453,10 @@ def tile_mlaselfattn_t_kernel(tc, x, cos, sin, Wqa, Wqb, Wkva, out):
         sa(2, 3)
         vqa(2, 3)
         vqx(3, 1)
-        txb(4, 0, 0, "S")
-        txb(4, 0, 1, "S")
-        txb(4, 1, 0, "S")
-        txb(4, 1, 1, "S")
+        tx(4, 0, "S")
+        tx(4, 1, "S")
+        tx(4, 2, "S")
+        tx(4, 3, "S")
         q(2)
         sn(2, 0)
         sn(2, 1)
@@ -449,10 +482,10 @@ def tile_mlaselfattn_t_kernel(tc, x, cos, sin, Wqa, Wqb, Wkva, out):
         sa(3, 3)
         vqa(3, 3)
         vqx(4, 1)
-        txb(5, 0, 0, "S")
-        txb(5, 0, 1, "S")
-        txb(5, 1, 0, "S")
-        txb(5, 1, 1, "S")
+        tx(5, 0, "S")
+        tx(5, 1, "S")
+        tx(5, 2, "S")
+        tx(5, 3, "S")
         q(3)
         sn(3, 0)
         sn(3, 1)
@@ -478,10 +511,10 @@ def tile_mlaselfattn_t_kernel(tc, x, cos, sin, Wqa, Wqb, Wkva, out):
         sa(4, 3)
         vqa(4, 3)
         vqx(5, 1)
-        txb(6, 0, 0, "S")
-        txb(6, 0, 1, "S")
-        txb(6, 1, 0, "S")
-        txb(6, 1, 1, "S")
+        tx(6, 0, "S")
+        tx(6, 1, "S")
+        tx(6, 2, "S")
+        tx(6, 3, "S")
         q(4)
         sn(4, 0)
         sn(4, 1)
@@ -507,18 +540,18 @@ def tile_mlaselfattn_t_kernel(tc, x, cos, sin, Wqa, Wqb, Wkva, out):
         sa(5, 3)
         vqa(5, 3)
         vqx(6, 1)
-        txb(7, 0, 0, "S")
-        txb(7, 0, 1, "S")
-        txb(7, 1, 0, "S")
-        txb(7, 1, 1, "S")
+        tx(7, 0, "S")
+        tx(7, 1, "S")
+        tx(7, 2, "S")
+        tx(7, 3, "S")
         q(5)
         sn(5, 0)
         sn(5, 1)
         k(6, 0)
         k(6, 1)
+        vqx(7, 0)
         ab(5, 0, 4)
         ck(5, "G")
-        vqx(7, 0)
         cq(5, 0, 4, "V")
         store(5, [0, 1], ["q", "kv"])
         a(6, 0)
@@ -527,6 +560,7 @@ def tile_mlaselfattn_t_kernel(tc, x, cos, sin, Wqa, Wqb, Wkva, out):
         vqa(6, 0)
         a(6, 1)
         sa(6, 1)
+        vqx(7, 1)
         vk(6, 1)
         vqa(6, 1)
         a(6, 2)
@@ -535,40 +569,43 @@ def tile_mlaselfattn_t_kernel(tc, x, cos, sin, Wqa, Wqb, Wkva, out):
         a(6, 3)
         sa(6, 3)
         vqa(6, 3)
+        k(7, 0)
+        ck(6, "G")
+        store(6, [0, 1], ["kv"])
         a(7, 0)
         sa(7, 0)
+        vk(7, 0)
+        k(7, 1)
+        vqa(7, 0)
         a(7, 1)
         sa(7, 1)
-        vqx(7, 1)
-        q(6)
+        vk(7, 1)
+        qpair(6, 0)
         sn(6, 0)
-        sn(6, 1)
-        ck(6, "V")
+        ck(7, "G")
+        store(7, [0, 1], ["kv"])
         a(7, 2)
         sa(7, 2)
-        k(7, 0)
+        ab(6, 0, 2)
+        vqa(7, 1)
+        cq(6, 0, 2, "G")
+        store(6, [0], ["q"])
+        qpair(6, 1)
         a(7, 3)
         sa(7, 3)
-        ab(6, 0, 4)
-        cq(6, 0, 4, "V")
-        vqa(7, 0)
-        vqa(7, 1)
+        sn(6, 1)
+        ab(6, 2, 2)
         vqa(7, 2)
-        vk(7, 0)
+        cq(6, 2, 2, "V")
         vqa(7, 3)
-        store(6, [0, 1], ["q", "kv"])
-        k(7, 1)
+        store(6, [1], ["q"])
         qpair(7, 0)
-        qpair(7, 1)
-        ckp(7, 0, "G")
         sn(7, 0)
         ab(7, 0, 2)
         cq(7, 0, 2, "V")
-        store(7, [0], ["q", "kv"])
-        vk(7, 1)
-        ab(7, 2, 2)
-        ckp(7, 1, "G")
+        store(7, [0], ["q"])
+        qpair(7, 1)
         sn(7, 1)
+        ab(7, 2, 2)
         cq(7, 2, 2, "V")
-        store(7, [1], ["kv"])
         store(7, [1], ["q"])

@@ -52,6 +52,8 @@ def tile_mlaselfattn_t_kernel(tc, x, cos, sin, Wqa, Wqb, Wkva, out):
         ident = const.tile([P, P], F32, name="ident", tag="ident")
         x_sb = [xpool.tile([P, TILES, HIDDEN], BF16, name="x%d" % r, tag="x") for r in range(ROUNDS)]
 
+        warm_sb = const.tile([P, 512], BF16, name="warm_sb", tag="warm_sb")
+        nc.vector.memset(warm_sb[:], 0.0)
         make_identity(nc, ident[:])
 
         def load(what):
@@ -77,6 +79,14 @@ def tile_mlaselfattn_t_kernel(tc, x, cos, sin, Wqa, Wqb, Wkva, out):
 
         def new_bank(nm):
             return psum.tile([P, 512], F32, name=nm, tag="bank")
+
+        warm_bank = {}
+
+        def warm(n):
+            if 0 not in warm_bank:
+                warm_bank[0] = new_bank("warm")
+            for d in range(n):
+                nc.tensor.matmul(out=warm_bank[0][:], lhsT=warm_sb[:, 0:P], rhs=warm_sb[:], start=True, stop=True)
 
         def transpose_bank(nm, blocks, g):
             n = len(blocks) * P
@@ -347,22 +357,27 @@ def tile_mlaselfattn_t_kernel(tc, x, cos, sin, Wqa, Wqb, Wkva, out):
         load("x5")
         load("x6")
         load("x7")
+        warm(8)
         wqa_t(0, "S")
         wqa_q(0)
         wqa_t(1, "V")
+        warm(1)
         wqa_q(1)
         wqa_t(2, "S")
         wqa_q(2)
         wqa_t(3, "V")
+        warm(1)
         wqa_q(3)
         tx(0, 0, "S")
         vqt(0, 0)
         tx(0, 1, "later")
+        warm(1)
         vx(0, 1)
         vqt(0, 1)
         tx(0, 2, "S")
         vqt(0, 2)
         tx(0, 3, "later")
+        warm(3)
         vx(0, 3)
         vqt(0, 3)
         a(0, 0)
@@ -383,6 +398,7 @@ def tile_mlaselfattn_t_kernel(tc, x, cos, sin, Wqa, Wqb, Wkva, out):
         wkv_q()
         wqb_t(0, "V")
         wqb_t(1, "V")
+        warm(2)
         wqb_q(0)
         wqb_q(1)
         tx(1, 0, "S")

@@ -39,8 +39,8 @@ def tile_mlaselfattn_t_kernel(tc, x, cos, sin, Wqa, Wqb, Wkva, out):
 
         xv = x.flatten_outer_dims().rearrange("(p r i) k -> p r (i k)", p=P, r=ROUNDS, i=TILES)
         ov = out.flatten_outer_dims().rearrange("(p r i) c -> p r i c", p=P, r=ROUNDS, i=TILES)
-        cosv = cos.flatten_outer_dims().rearrange("(p t) c -> p (t c)", p=P)
-        sinv = sin.flatten_outer_dims().rearrange("(p t) c -> p (t c)", p=P)
+        cosv = cos.flatten_outer_dims().rearrange("(p t) c -> p t c", p=P)
+        sinv = sin.flatten_outer_dims().rearrange("(p t) c -> p t c", p=P)
         wqa_v = Wqa.rearrange("(u p e) k -> p u e k", u=2, p=P, e=2)
 
         wqa_raw = const.tile([P, 4, HIDDEN], BF16, name="wqa_raw", tag="wqa_raw")
@@ -52,9 +52,10 @@ def tile_mlaselfattn_t_kernel(tc, x, cos, sin, Wqa, Wqb, Wkva, out):
         ident = const.tile([P, P], F32, name="ident", tag="ident")
         x_sb = [xpool.tile([P, TILES, HIDDEN], BF16, name="x%d" % r, tag="x") for r in range(ROUNDS)]
 
-        warm_sb = const.tile([P, 512], BF16, name="warm_sb", tag="warm_sb")
-        nc.vector.memset(warm_sb[:], 0.0)
         make_identity(nc, ident[:])
+
+        def part(ab_):
+            return slice(0, 8) if ab_ == "A" else slice(8, 32)
 
         def load(what):
             if what[0:3] == "wqa":
@@ -69,24 +70,16 @@ def tile_mlaselfattn_t_kernel(tc, x, cos, sin, Wqa, Wqb, Wkva, out):
                 nc.sync.dma_start(out=wqb_raw[:, 0:2, :], in_=Wqb.rearrange("(h r) k -> r h k", h=2)[0:128, :, :])
                 nc.sync.dma_start(out=wqb_raw[0:64, 2, :], in_=Wqb[128:192, :])
                 nc.sync.dma_start(out=wqb_raw[64:128, 2, :], in_=Wqb[320:384, :])
-            elif what == "cos":
-                nc.sync.dma_start(out=cos_sb[:].rearrange("p t c -> p (t c)"), in_=cosv)
-            elif what == "sin":
-                nc.sync.dma_start(out=sin_sb[:].rearrange("p t c -> p (t c)"), in_=sinv)
+            elif what[0:3] == "cos":
+                nc.sync.dma_start(out=cos_sb[:, part(what[3]), :], in_=cosv[:, part(what[3]), :])
+            elif what[0:3] == "sin":
+                nc.sync.dma_start(out=sin_sb[:, part(what[3]), :], in_=sinv[:, part(what[3]), :])
             else:
                 r = int(what[1:])
                 nc.sync.dma_start(out=x_sb[r][:].rearrange("p i k -> p (i k)"), in_=xv[:, r, :])
 
         def new_bank(nm):
             return psum.tile([P, 512], F32, name=nm, tag="bank")
-
-        warm_bank = {}
-
-        def warm(n):
-            if 0 not in warm_bank:
-                warm_bank[0] = new_bank("warm")
-            for d in range(n):
-                nc.tensor.matmul(out=warm_bank[0][:], lhsT=warm_sb[:, 0:P], rhs=warm_sb[:], start=True, stop=True)
 
         def transpose_bank(nm, blocks, g):
             n = len(blocks) * P
@@ -174,9 +167,9 @@ def tile_mlaselfattn_t_kernel(tc, x, cos, sin, Wqa, Wqb, Wkva, out):
             c = slice(0, 256) if b == 0 else slice(256, 384)
             quant(wqb_c[:, c], wqb_s[:, c], wqb_g[:, c, :].rearrange("p n t -> p (n t)"))
 
-        def sinx():
-            nc.vector.tensor_copy(out=sinx_sb[:, :, 0:32], in_=sin_sb[:, :, 32:64])
-            nc.vector.tensor_copy(out=sinx_sb[:, :, 32:64], in_=sin_sb[:, :, 0:32])
+        def sinx(ab_):
+            nc.vector.tensor_copy(out=sinx_sb[:, part(ab_), 0:32], in_=sin_sb[:, part(ab_), 32:64])
+            nc.vector.tensor_copy(out=sinx_sb[:, part(ab_), 32:64], in_=sin_sb[:, part(ab_), 0:32])
 
         xg = {}
         xsrc = {}
@@ -348,38 +341,42 @@ def tile_mlaselfattn_t_kernel(tc, x, cos, sin, Wqa, Wqb, Wkva, out):
         load("x0t3")
         load("wkv")
         load("wqb")
-        load("sin")
+        load("sinA")
+        load("cosA")
         load("x1")
-        load("cos")
         load("x2")
         load("x3")
+        load("sinB")
+        load("cosB")
         load("x4")
         load("x5")
         load("x6")
         load("x7")
-        warm(8)
         wqa_t(0, "S")
         wqa_q(0)
         wqa_t(1, "V")
-        warm(1)
         wqa_q(1)
         wqa_t(2, "S")
         wqa_q(2)
         wqa_t(3, "V")
-        warm(1)
         wqa_q(3)
         tx(0, 0, "S")
         vqt(0, 0)
         tx(0, 1, "later")
-        warm(1)
         vx(0, 1)
         vqt(0, 1)
         tx(0, 2, "S")
         vqt(0, 2)
         tx(0, 3, "later")
-        warm(3)
         vx(0, 3)
         vqt(0, 3)
+        wkv_t(0, "S")
+        wkv_t(1, "V")
+        wqb_t(0, "S")
+        wqb_t(1, "V")
+        wkv_q()
+        wqb_q(0)
+        wqb_q(1)
         a(0, 0)
         sa(0, 0)
         vqa(0, 0)
@@ -389,18 +386,10 @@ def tile_mlaselfattn_t_kernel(tc, x, cos, sin, Wqa, Wqb, Wkva, out):
         a(0, 2)
         sa(0, 2)
         vqa(0, 2)
-        sinx()
+        sinx("A")
         a(0, 3)
         sa(0, 3)
         vqa(0, 3)
-        wkv_t(0, "S")
-        wkv_t(1, "V")
-        wkv_q()
-        wqb_t(0, "V")
-        wqb_t(1, "V")
-        warm(2)
-        wqb_q(0)
-        wqb_q(1)
         tx(1, 0, "S")
         tx(1, 1, "S")
         tx(1, 2, "S")
@@ -439,6 +428,7 @@ def tile_mlaselfattn_t_kernel(tc, x, cos, sin, Wqa, Wqb, Wkva, out):
         a(1, 3)
         sa(1, 3)
         vqa(1, 3)
+        sinx("B")
         vqx(2, 1)
         tx(3, 0, "S")
         tx(3, 1, "S")

@@ -408,23 +408,23 @@ def tile_mlaselfattn_t_kernel(tc, x, cos, sin, Wqa, Wqb, Wkva, out):
         sn(0, 0)
         sn(0, 1)
         k(1, 0)
+        a(1, 0)
         k(1, 1)
         ab(0, 0, 4)
-        ck(0, "V")
-        cq(0, 0, 4, "V")
-        store(0, [0, 1], ["q", "kv"])
-        a(1, 0)
-        sa(1, 0)
         vk(1, 0)
+        ck(0, "G")
+        cq(0, 0, 4, "G")
+        vk(1, 1)
+        store(0, [0, 1], ["q", "kv"])
+        sa(1, 0)
         vqa(1, 0)
         a(1, 1)
         sa(1, 1)
-        vk(1, 1)
         vqa(1, 1)
+        vqx(2, 0)
         a(1, 2)
         sa(1, 2)
         vqa(1, 2)
-        vqx(2, 0)
         a(1, 3)
         sa(1, 3)
         vqa(1, 3)
@@ -438,23 +438,23 @@ def tile_mlaselfattn_t_kernel(tc, x, cos, sin, Wqa, Wqb, Wkva, out):
         sn(1, 0)
         sn(1, 1)
         k(2, 0)
+        a(2, 0)
         k(2, 1)
         ab(1, 0, 4)
-        ck(1, "V")
-        cq(1, 0, 4, "V")
-        store(1, [0, 1], ["q", "kv"])
-        a(2, 0)
-        sa(2, 0)
         vk(2, 0)
+        ck(1, "G")
+        cq(1, 0, 4, "G")
+        vk(2, 1)
+        store(1, [0, 1], ["q", "kv"])
+        sa(2, 0)
         vqa(2, 0)
         a(2, 1)
         sa(2, 1)
-        vk(2, 1)
         vqa(2, 1)
+        vqx(3, 0)
         a(2, 2)
         sa(2, 2)
         vqa(2, 2)
-        vqx(3, 0)
         a(2, 3)
         sa(2, 3)
         vqa(2, 3)
@@ -467,23 +467,23 @@ def tile_mlaselfattn_t_kernel(tc, x, cos, sin, Wqa, Wqb, Wkva, out):
         sn(2, 0)
         sn(2, 1)
         k(3, 0)
+        a(3, 0)
         k(3, 1)
         ab(2, 0, 4)
-        ck(2, "V")
-        cq(2, 0, 4, "V")
-        store(2, [0, 1], ["q", "kv"])
-        a(3, 0)
-        sa(3, 0)
         vk(3, 0)
+        ck(2, "G")
+        cq(2, 0, 4, "G")
+        vk(3, 1)
+        store(2, [0, 1], ["q", "kv"])
+        sa(3, 0)
         vqa(3, 0)
         a(3, 1)
         sa(3, 1)
-        vk(3, 1)
         vqa(3, 1)
+        vqx(4, 0)
         a(3, 2)
         sa(3, 2)
         vqa(3, 2)
-        vqx(4, 0)
         a(3, 3)
         sa(3, 3)
         vqa(3, 3)
@@ -496,23 +496,23 @@ def tile_mlaselfattn_t_kernel(tc, x, cos, sin, Wqa, Wqb, Wkva, out):
         sn(3, 0)
         sn(3, 1)
         k(4, 0)
+        a(4, 0)
         k(4, 1)
         ab(3, 0, 4)
-        ck(3, "V")
-        cq(3, 0, 4, "V")
-        store(3, [0, 1], ["q", "kv"])
-        a(4, 0)
-        sa(4, 0)
         vk(4, 0)
+        ck(3, "G")
+        cq(3, 0, 4, "G")
+        vk(4, 1)
+        store(3, [0, 1], ["q", "kv"])
+        sa(4, 0)
         vqa(4, 0)
         a(4, 1)
         sa(4, 1)
-        vk(4, 1)
         vqa(4, 1)
+        vqx(5, 0)
         a(4, 2)
         sa(4, 2)
         vqa(4, 2)
-        vqx(5, 0)
         a(4, 3)
         sa(4, 3)
         vqa(4, 3)
@@ -525,23 +525,23 @@ def tile_mlaselfattn_t_kernel(tc, x, cos, sin, Wqa, Wqb, Wkva, out):
         sn(4, 0)
         sn(4, 1)
         k(5, 0)
+        a(5, 0)
         k(5, 1)
         ab(4, 0, 4)
-        ck(4, "V")
-        cq(4, 0, 4, "V")
-        store(4, [0, 1], ["q", "kv"])
-        a(5, 0)
-        sa(5, 0)
         vk(5, 0)
+        ck(4, "G")
+        cq(4, 0, 4, "G")
+        vk(5, 1)
+        store(4, [0, 1], ["q", "kv"])
+        sa(5, 0)
         vqa(5, 0)
         a(5, 1)
         sa(5, 1)
-        vk(5, 1)
         vqa(5, 1)
+        vqx(6, 0)
         a(5, 2)
         sa(5, 2)
         vqa(5, 2)
-        vqx(6, 0)
         a(5, 3)
         sa(5, 3)
         vqa(5, 3)
@@ -557,16 +557,16 @@ def tile_mlaselfattn_t_kernel(tc, x, cos, sin, Wqa, Wqb, Wkva, out):
         k(6, 1)
         vqx(7, 0)
         ab(5, 0, 4)
+        vk(6, 0)
         ck(5, "G")
         cq(5, 0, 4, "V")
         store(5, [0, 1], ["q", "kv"])
+        vqx(7, 1)
         a(6, 0)
         sa(6, 0)
-        vk(6, 0)
         vqa(6, 0)
         a(6, 1)
         sa(6, 1)
-        vqx(7, 1)
         vk(6, 1)
         vqa(6, 1)
         a(6, 2)

@@ -52,6 +52,8 @@ def tile_mlaselfattn_t_kernel(tc, x, cos, sin, Wqa, Wqb, Wkva, out):
         ident = const.tile([P, P], F32, name="ident", tag="ident")
         x_sb = [xpool.tile([P, TILES, HIDDEN], BF16, name="x%d" % r, tag="x") for r in range(ROUNDS)]
 
+        warm_sb = const.tile([P, 512], BF16, name="warm_sb", tag="warm_sb")
+        nc.vector.memset(warm_sb[:], 0.0)
         make_identity(nc, ident[:])
 
         def part(ab_):
@@ -80,6 +82,14 @@ def tile_mlaselfattn_t_kernel(tc, x, cos, sin, Wqa, Wqb, Wkva, out):
 
         def new_bank(nm):
             return psum.tile([P, 512], F32, name=nm, tag="bank")
+
+        warm_bank = {}
+
+        def warm(n):
+            if 0 not in warm_bank:
+                warm_bank[0] = new_bank("warm")
+            for d in range(n):
+                nc.tensor.matmul(out=warm_bank[0][:], lhsT=warm_sb[:, 0:P], rhs=warm_sb[:], start=True, stop=True)
 
         def transpose_bank(nm, blocks, g):
             n = len(blocks) * P
@@ -352,28 +362,35 @@ def tile_mlaselfattn_t_kernel(tc, x, cos, sin, Wqa, Wqb, Wkva, out):
         load("x5")
         load("x6")
         load("x7")
+        warm(8)
         wqa_t(0, "S")
         wqa_q(0)
         wqa_t(1, "V")
+        warm(1)
         wqa_q(1)
         wqa_t(2, "S")
         wqa_q(2)
         wqa_t(3, "V")
+        warm(1)
         wqa_q(3)
         tx(0, 0, "S")
         vqt(0, 0)
         tx(0, 1, "later")
+        warm(1)
         vx(0, 1)
         vqt(0, 1)
         tx(0, 2, "S")
         vqt(0, 2)
         tx(0, 3, "later")
+        warm(1)
         vx(0, 3)
         vqt(0, 3)
         wkv_t(0, "S")
         wkv_t(1, "V")
+        warm(1)
         wqb_t(0, "S")
         wqb_t(1, "V")
+        warm(1)
         wkv_q()
         wqb_q(0)
         wqb_q(1)

@@ -449,7 +449,8 @@ def tile_mlaselfattn_t_kernel(tc, x, cos, sin, Wqa, Wqb, Wkva, out):
         vqx(2, 1)
         tx(3, 0, "S")
         tx(3, 1, "S")
-        tx(3, 2, "S")
+        tx(3, 2, "later")
+        vx(3, 2)
         tx(3, 3, "S")
         q(1)
         sn(1, 0)
@@ -478,7 +479,8 @@ def tile_mlaselfattn_t_kernel(tc, x, cos, sin, Wqa, Wqb, Wkva, out):
         vqx(3, 1)
         tx(4, 0, "S")
         tx(4, 1, "S")
-        tx(4, 2, "S")
+        tx(4, 2, "later")
+        vx(4, 2)
         tx(4, 3, "S")
         q(2)
         sn(2, 0)
@@ -507,7 +509,8 @@ def tile_mlaselfattn_t_kernel(tc, x, cos, sin, Wqa, Wqb, Wkva, out):
         vqx(4, 1)
         tx(5, 0, "S")
         tx(5, 1, "S")
-        tx(5, 2, "S")
+        tx(5, 2, "later")
+        vx(5, 2)
         tx(5, 3, "S")
         q(3)
         sn(3, 0)
@@ -536,7 +539,8 @@ def tile_mlaselfattn_t_kernel(tc, x, cos, sin, Wqa, Wqb, Wkva, out):
         vqx(5, 1)
         tx(6, 0, "S")
         tx(6, 1, "S")
-        tx(6, 2, "S")
+        tx(6, 2, "later")
+        vx(6, 2)
         tx(6, 3, "S")
         q(4)
         sn(4, 0)
@@ -565,7 +569,8 @@ def tile_mlaselfattn_t_kernel(tc, x, cos, sin, Wqa, Wqb, Wkva, out):
         vqx(6, 1)
         tx(7, 0, "S")
         tx(7, 1, "S")
-        tx(7, 2, "S")
+        tx(7, 2, "later")
+        vx(7, 2)
         tx(7, 3, "S")
         q(5)
         sn(5, 0)

from contextlib import ExitStack

import concourse.mybir as mybir
from concourse.masks import make_identity

F32 = mybir.dt.float32
BF16 = mybir.dt.bfloat16
U32 = mybir.dt.uint32
U8 = mybir.dt.uint8
FP8X4 = mybir.dt.float8_e4m3fn_x4
MULT = mybir.AluOpType.mult
ADD = mybir.AluOpType.add
SUB = mybir.AluOpType.subtract

P = 128
TOKENS = 4096
HIDDEN = 1024
Q_LORA = 512
ROUNDS = 8
TILES = 4
OUT_W = 640

FLOPS = 2 * TOKENS * (HIDDEN * 768 + Q_LORA * 384)


def tile_mlaselfattn_t_kernel(tc, x, cos, sin, Wqa, Wqb, Wkva, out):
    nc = tc.nc
    with ExitStack() as ctx:
        ctx.enter_context(tc.manual_schedule())
        const = ctx.enter_context(tc.tile_pool(name="const", bufs=1))
        xpool = ctx.enter_context(tc.tile_pool(name="xpool", bufs=ROUNDS))
        xgp = ctx.enter_context(tc.tile_pool(name="xgp", bufs=6))
        xcp = ctx.enter_context(tc.tile_pool(name="xcp", bufs=6))
        qgp = ctx.enter_context(tc.tile_pool(name="qgp", bufs=4))
        qcp = ctx.enter_context(tc.tile_pool(name="qcp", bufs=10))
        outp = ctx.enter_context(tc.tile_pool(name="outp", bufs=4))
        tmpp = ctx.enter_context(tc.tile_pool(name="tmpp", bufs=3))
        psum = ctx.enter_context(tc.psum_pool(name="psum", bufs=8))

        xv = x.flatten_outer_dims().rearrange("(p r i) k -> p r (i k)", p=P, r=ROUNDS, i=TILES)
        ov = out.flatten_outer_dims().rearrange("(p r i) c -> p r i c", p=P, r=ROUNDS, i=TILES)
        cosv = cos.flatten_outer_dims().rearrange("(p t) c -> p t c", p=P)
        sinv = sin.flatten_outer_dims().rearrange("(p t) c -> p t c", p=P)
        wqa_v = Wqa.rearrange("(u p e) k -> p u e k", u=2, p=P, e=2)

        wqa_raw = const.tile([P, 4, HIDDEN], BF16, name="wqa_raw", tag="wqa_raw")
        wkv_raw = const.tile([P, 2, HIDDEN], BF16, name="wkv_raw", tag="wkv_raw")
        wqb_raw = const.tile([P, 3, Q_LORA], BF16, name="wqb_raw", tag="wqb_raw")
        cos_sb = const.tile([P, 32, 64], BF16, name="cos_sb", tag="cos_sb")
        sin_sb = const.tile([P, 32, 64], BF16, name="sin_sb", tag="sin_sb")
        sinx_sb = const.tile([P, 32, 64], BF16, name="sinx_sb", tag="sinx_sb")
        ident = const.tile([P, P], F32, name="ident", tag="ident")
        x_sb = [xpool.tile([P, TILES, HIDDEN], BF16, name="x%d" % r, tag="x") for r in range(ROUNDS)]

        warm_sb = const.tile([P, 512], BF16, name="warm_sb", tag="warm_sb")
        nc.vector.memset(warm_sb[:], 0.0)
        make_identity(nc, ident[:])

        def part(ab_):
            return slice(0, 8) if ab_ == "A" else slice(8, 32)

        def load(what):
            if what[0:3] == "wqa":
                j = int(what[3:])
                nc.sync.dma_start(out=wqa_raw[:, j, :], in_=wqa_v[:, j // 2, j % 2, :])
            elif what[0:3] == "x0t":
                i = int(what[3:])
                nc.sync.dma_start(out=x_sb[0][:, i, :], in_=xv[:, 0, i * HIDDEN : (i + 1) * HIDDEN])
            elif what == "wkv":
                nc.sync.dma_start(out=wkv_raw[:], in_=Wkva.rearrange("(b p) k -> p b k", p=P))
            elif what == "wqb":
                nc.sync.dma_start(out=wqb_raw[:, 0:2, :], in_=Wqb.rearrange("(h r) k -> r h k", h=2)[0:128, :, :])
                nc.sync.dma_start(out=wqb_raw[0:64, 2, :], in_=Wqb[128:192, :])
                nc.sync.dma_start(out=wqb_raw[64:128, 2, :], in_=Wqb[320:384, :])
            elif what[0:3] == "cos":
                nc.sync.dma_start(out=cos_sb[:, part(what[3]), :], in_=cosv[:, part(what[3]), :])
            elif what[0:3] == "sin":
                nc.sync.dma_start(out=sin_sb[:, part(what[3]), :], in_=sinv[:, part(what[3]), :])
            else:
                r = int(what[1:])
                nc.sync.dma_start(out=x_sb[r][:].rearrange("p i k -> p (i k)"), in_=xv[:, r, :])

        def new_bank(nm):
            return psum.tile([P, 512], F32, name=nm, tag="bank")

        warm_bank = {}

        def warm(n):
            if 0 not in warm_bank:
                warm_bank[0] = new_bank("warm")
            for d in range(n):
                nc.tensor.matmul(out=warm_bank[0][:], lhsT=warm_sb[:, 0:P], rhs=warm_sb[:], start=True, stop=True)

        def transpose_bank(nm, blocks, g):
            n = len(blocks) * P
            bank = new_bank(nm)
            for u in range(2):
                for b in range(len(blocks)):
                    w0 = 256 * g + 128 * u
                    nc.tensor.transpose(
                        out=bank[:, u * n + b * P : u * n + (b + 1) * P],
                        in_=blocks[b].bitcast(F32)[:, w0 : w0 + P],
                        identity=ident[:],
                    )
            return bank[:, 0 : 2 * n].rearrange("p (u n) -> p n u", u=2)

        def copy_out(eng, dst, src):
            if eng == "S":
                nc.scalar.copy(out=dst, in_=src)
            else:
                nc.vector.tensor_copy(out=dst, in_=src)

        def drain_words(eng, grouped2d, src):
            copy_out(eng, grouped2d.bitcast(F32).rearrange("p (n u) -> p n u", u=2), src)

        def transpose_rows(nm, block):
            bank = new_bank(nm)
            for w in range(4):
                nc.tensor.transpose(
                    out=bank[:, w * P : (w + 1) * P], in_=block.bitcast(F32)[:, w * P : (w + 1) * P], identity=ident[:]
                )
            return bank[:].rearrange("p (g u n) -> p g n u", g=2, u=2)

        def drain_rows(eng, grouped2d, src):
            copy_out(eng, grouped2d.bitcast(F32).rearrange("p (g n u) -> p g n u", g=2, u=2), src)

        def quant(codes, scales, grouped2d):
            nc.vector.quantize_mx(out=codes.bitcast(FP8X4), scales=scales, in_=grouped2d)

        def mx(o, l, ls, r_, rs, start, stop):
            nc.tensor.matmul_mx(
                out=o, lhsT=l.bitcast(FP8X4), lhsT_scale=ls, rhs=r_.bitcast(FP8X4), rhs_scale=rs,
                start=start, stop=stop,
            )

        wqa_g = const.tile([P, 4, 2, P, 4], BF16, name="wqa_g", tag="wqa_g", align_bytes=64)
        wqa_c = const.tile([P, 4, 2, P], U32, name="wqa_c", tag="wqa_c", align_bytes=64)
        wqa_s = const.tile([P, 4, 2, P], U8, name="wqa_s", tag="wqa_s", align_bytes=64)
        wkv_g = const.tile([P, 2, 256, 4], BF16, name="wkv_g", tag="wkv_g", align_bytes=64)
        wkv_c = const.tile([P, 2, 256], U32, name="wkv_c", tag="wkv_c", align_bytes=64)
        wkv_s = const.tile([P, 2, 256], U8, name="wkv_s", tag="wkv_s", align_bytes=64)
        wqb_g = const.tile([P, 384, 4], BF16, name="wqb_g", tag="wqb_g", align_bytes=64)
        wqb_c = const.tile([P, 384], U32, name="wqb_c", tag="wqb_c", align_bytes=64)
        wqb_s = const.tile([P, 384], U8, name="wqb_s", tag="wqb_s", align_bytes=64)

        def wqa_t(j, eng):
            src = transpose_rows("wa%d" % j, wqa_raw[:, j, :])
            drain_rows(eng, wqa_g[:, j, :, :, :].rearrange("p g n t -> p (g n t)"), src)

        def wqa_q(j):
            quant(
                wqa_c[:, j, :, :].rearrange("p g n -> p (g n)"),
                wqa_s[:, j, :, :].rearrange("p g n -> p (g n)"),
                wqa_g[:, j, :, :, :].rearrange("p g n t -> p (g n t)"),
            )

        def wkv_t(g, eng):
            src = transpose_bank("wk%d" % g, [wkv_raw[:, 0, :], wkv_raw[:, 1, :]], g)
            drain_words(eng, wkv_g[:, g, :, :].rearrange("p n t -> p (n t)"), src)

        def wkv_q():
            quant(
                wkv_c[:].rearrange("p g n -> p (g n)"),
                wkv_s[:].rearrange("p g n -> p (g n)"),
                wkv_g[:].rearrange("p g n t -> p (g n t)"),
            )

        def wqb_t(b, eng):
            if b == 0:
                src = transpose_bank("wb0", [wqb_raw[:, 0, :], wqb_raw[:, 1, :]], 0)
                drain_words(eng, wqb_g[:, 0:256, :].rearrange("p n t -> p (n t)"), src)
            else:
                src = transpose_bank("wb1", [wqb_raw[:, 2, :]], 0)
                drain_words(eng, wqb_g[:, 256:384, :].rearrange("p n t -> p (n t)"), src)

        def wqb_q(b):
            c = slice(0, 256) if b == 0 else slice(256, 384)
            quant(wqb_c[:, c], wqb_s[:, c], wqb_g[:, c, :].rearrange("p n t -> p (n t)"))

        def sinx(ab_):
            nc.vector.tensor_copy(out=sinx_sb[:, part(ab_), 0:32], in_=sin_sb[:, part(ab_), 32:64])
            nc.vector.tensor_copy(out=sinx_sb[:, part(ab_), 32:64], in_=sin_sb[:, part(ab_), 0:32])

        xg = {}
        xsrc = {}
        xc = {}
        xs = {}
        qbank = {}
        qg = {}
        qc = {}
        qs = {}
        kbank = {}
        nbank = {}
        pbank = {}
        osb = {}
        tk = {}
        tq = {}

        def xdst(r, i):
            return xg[(r, i // 2)][:, i % 2, :, :, :].rearrange("p g n t -> p (g n t)")

        def tx(r, i, eng):
            if (r, i // 2) not in xg:
                xg[(r, i // 2)] = xgp.tile([P, 2, 2, P, 4], BF16, name="xg%d_%d" % (r, i // 2), tag="xg", align_bytes=64)
            xsrc[(r, i)] = transpose_rows("xt%d_%d" % (r, i), x_sb[r][:, i, :])
            if eng == "S":
                drain_rows("S", xdst(r, i), xsrc[(r, i)])

        def vx(r, i):
            drain_rows("V", xdst(r, i), xsrc[(r, i)])

        def new_codes(r, pr):
            if (r, pr) not in xc:
                xc[(r, pr)] = xcp.tile([P, 2, 2, P], U32, name="xc%d_%d" % (r, pr), tag="xc", align_bytes=64)
                xs[(r, pr)] = xcp.tile([P, 2, 2, P], U8, name="xs%d_%d" % (r, pr), tag="xs", align_bytes=64)

        def vqx(r, pr):
            new_codes(r, pr)
            quant(
                xc[(r, pr)][:].rearrange("p i g n -> p (i g n)"),
                xs[(r, pr)][:].rearrange("p i g n -> p (i g n)"),
                xg[(r, pr)][:].rearrange("p i g n t -> p (i g n t)"),
            )

        def vqt(r, i):
            new_codes(r, i // 2)
            quant(
                xc[(r, i // 2)][:, i % 2, :, :].rearrange("p g n -> p (g n)"),
                xs[(r, i // 2)][:, i % 2, :, :].rearrange("p g n -> p (g n)"),
                xdst(r, i),
            )

        def a(r, i):
            pr, i2 = i // 2, i % 2
            bank = new_bank("qa%d_%d" % (r, i))
            qbank[(r, i)] = bank
            for j in range(4):
                for g in range(2):
                    mx(
                        bank[:, j * P : (j + 1) * P],
                        wqa_c[:, j, g, :], wqa_s[:, j, g, :],
                        xc[(r, pr)][:, i2, g, :], xs[(r, pr)][:, i2, g, :],
                        g == 0, g == 1,
                    )

        def sa(r, i):
            qg[(r, i)] = qgp.tile([P, P, 4], BF16, name="qg%d_%d" % (r, i), tag="qg", align_bytes=64)
            nc.scalar.copy(out=qg[(r, i)][:], in_=qbank[(r, i)][:].rearrange("p (j n) -> p n j", j=4))

        def vqa(r, i):
            qc[(r, i)] = qcp.tile([P, P], U32, name="qc%d_%d" % (r, i), tag="qc", align_bytes=64)
            qs[(r, i)] = qcp.tile([P, P], U8, name="qs%d_%d" % (r, i), tag="qs", align_bytes=64)
            quant(qc[(r, i)][:], qs[(r, i)][:], qg[(r, i)][:].rearrange("p n t -> p (n t)"))

        def k(r, pr):
            bank = new_bank("kv%d_%d" % (r, pr))
            kbank[(r, pr)] = bank
            for i2 in range(2):
                for g in range(2):
                    mx(
                        bank[:, i2 * 256 : (i2 + 1) * 256],
                        xc[(r, pr)][:, i2, g, :], xs[(r, pr)][:, i2, g, :],
                        wkv_c[:, g, :], wkv_s[:, g, :],
                        g == 0, g == 1,
                    )

        def q_pass(r, i, nb, ncol, pb, pcol):
            mx(nb[:, ncol : ncol + 256], qc[(r, i)][:], qs[(r, i)][:], wqb_c[:, 0:256], wqb_s[:, 0:256], True, True)
            mx(pb[:, pcol : pcol + P], qc[(r, i)][:], qs[(r, i)][:], wqb_c[:, 256:384], wqb_s[:, 256:384], True, True)

        def q(r):
            for pr in range(2):
                nbank[(r, pr)] = new_bank("qn%d_%d" % (r, pr))
                if pr == 0:
                    pbank[(r, 0)] = new_bank("qp%d" % r)
                for i2 in range(2):
                    i = 2 * pr + i2
                    q_pass(r, i, nbank[(r, pr)], i2 * 256, pbank[(r, 0)], i * P)

        def qpair(r, pr):
            nbank[(r, pr)] = new_bank("qn%d_%d" % (r, pr))
            pbank[(r, 2 * pr)] = new_bank("qp%d_%d" % (r, pr))
            for i2 in range(2):
                q_pass(r, 2 * pr + i2, nbank[(r, pr)], i2 * 256, pbank[(r, 2 * pr)], i2 * P)

        def get_o(r):
            if r not in osb:
                osb[r] = outp.tile([P, TILES, OUT_W], F32, name="o%d" % r, tag="o")
            return osb[r]

        def vk(r, pr):
            if r not in tk:
                tk[r] = tmpp.tile([P, TILES, 64], F32, name="tk%d" % r, tag="tk")
            kv = kbank[(r, pr)][:].rearrange("p (i c) -> p i c", i=2)
            o = get_o(r)
            t0 = TILES * r + 2 * pr
            rows = slice(2 * pr, 2 * pr + 2)
            nc.vector.tensor_tensor(out=o[:, rows, 384:448], in0=kv[:, :, 192:256], in1=cos_sb[:, t0 : t0 + 2, :], op=MULT)
            nc.vector.tensor_tensor(out=tk[r][:, rows, :], in0=kv[:, :, 192:256], in1=sinx_sb[:, t0 : t0 + 2, :], op=MULT)
            nc.vector.tensor_copy(out=o[:, rows, 448:640], in_=kv[:, :, 0:192])

        def sn(r, pr):
            o = get_o(r)[:, 2 * pr : 2 * pr + 2, 0:384].rearrange("p i (h c) -> p i h c", h=2)
            nc.scalar.copy(out=o[:, :, :, 0:128], in_=nbank[(r, pr)][:].rearrange("p (i h c) -> p i h c", i=2, h=2))

        def ab(r, i0, n):
            if r not in tq:
                tq[r] = tmpp.tile([P, TILES, 2, 64], F32, name="tq%d" % r, tag="tq")
            oq = get_o(r)[:, i0 : i0 + n, 0:384].rearrange("p i (h c) -> p i h c", h=2)
            pe = pbank[(r, i0)][:, 0 : n * P].rearrange("p (i h c) -> p i h c", i=n, h=2)
            t0 = TILES * r + i0
            cb = cos_sb[:, t0 : t0 + n, :].unsqueeze(2).to_broadcast([P, n, 2, 64])
            sb = sinx_sb[:, t0 : t0 + n, :].unsqueeze(2).to_broadcast([P, n, 2, 64])
            nc.vector.tensor_tensor(out=oq[:, :, :, 128:192], in0=pe, in1=cb, op=MULT)
            nc.vector.tensor_tensor(out=tq[r][:, i0 : i0 + n, :, :], in0=pe, in1=sb, op=MULT)

        def engine(e):
            return nc.gpsimd if e == "G" else nc.vector

        def ck_rows(r, rows, e):
            o = osb[r]
            engine(e).tensor_tensor(out=o[:, rows, 384:416], in0=o[:, rows, 384:416], in1=tk[r][:, rows, 32:64], op=SUB)
            engine(e).tensor_tensor(out=o[:, rows, 416:448], in0=o[:, rows, 416:448], in1=tk[r][:, rows, 0:32], op=ADD)

        def ck(r, e):
            ck_rows(r, slice(0, TILES), e)

        def ckp(r, pr, e):
            ck_rows(r, slice(2 * pr, 2 * pr + 2), e)

        def cq(r, i0, n, e):
            oq = osb[r][:, i0 : i0 + n, 0:384].rearrange("p i (h c) -> p i h c", h=2)
            t = tq[r][:, i0 : i0 + n, :, :]
            engine(e).tensor_tensor(out=oq[:, :, :, 128:160], in0=oq[:, :, :, 128:160], in1=t[:, :, :, 32:64], op=SUB)
            engine(e).tensor_tensor(out=oq[:, :, :, 160:192], in0=oq[:, :, :, 160:192], in1=t[:, :, :, 0:32], op=ADD)

        def store(r, prs, parts):
            i0 = 2 * prs[0]
            n = 2 * len(prs)
            c0 = 0 if "q" in parts else 384
            c1 = OUT_W if "kv" in parts else 384
            nc.sync.dma_start(out=ov[:, r, i0 : i0 + n, c0:c1], in_=osb[r][:, i0 : i0 + n, c0:c1])

        load("wqa0")
        load("wqa1")
        load("wqa2")
        load("wqa3")
        load("x0t0")
        load("x0t1")
        load("x0t2")
        load("x0t3")
        load("wkv")
        load("wqb")
        load("sinA")
        load("cosA")
        load("x1")
        load("x2")
        load("x3")
        load("sinB")
        load("cosB")
        load("x4")
        load("x5")
        load("x6")
        load("x7")
        warm(8)
        wqa_t(0, "S")
        wqa_q(0)
        wqa_t(1, "V")
        warm(1)
        wqa_q(1)
        wqa_t(2, "S")
        wqa_q(2)
        wqa_t(3, "V")
        warm(1)
        wqa_q(3)
        tx(0, 0, "S")
        vqt(0, 0)
        tx(0, 1, "later")
        warm(1)
        vx(0, 1)
        vqt(0, 1)
        tx(0, 2, "S")
        vqt(0, 2)
        tx(0, 3, "later")
        warm(1)
        vx(0, 3)
        vqt(0, 3)
        wkv_t(0, "S")
        wkv_t(1, "V")
        warm(1)
        wqb_t(0, "S")
        wqb_t(1, "V")
        warm(1)
        wkv_q()
        wqb_q(0)
        wqb_q(1)
        a(0, 0)
        sa(0, 0)
        vqa(0, 0)
        a(0, 1)
        sa(0, 1)
        vqa(0, 1)
        a(0, 2)
        sa(0, 2)
        vqa(0, 2)
        sinx("A")
        a(0, 3)
        sa(0, 3)
        vqa(0, 3)
        tx(1, 0, "S")
        tx(1, 1, "S")
        tx(1, 2, "S")
        tx(1, 3, "S")
        k(0, 0)
        k(0, 1)
        vk(0, 0)
        vqx(1, 0)
        vk(0, 1)
        vqx(1, 1)
        tx(2, 0, "S")
        tx(2, 1, "S")
        tx(2, 2, "S")
        tx(2, 3, "S")
        q(0)
        sn(0, 0)
        sn(0, 1)
        k(1, 0)
        a(1, 0)
        k(1, 1)
        ab(0, 0, 4)
        vk(1, 0)
        ck(0, "G")
        cq(0, 0, 4, "G")
        vk(1, 1)
        store(0, [0, 1], ["q", "kv"])
        sa(1, 0)
        vqa(1, 0)
        a(1, 1)
        sa(1, 1)
        vqa(1, 1)
        vqx(2, 0)
        a(1, 2)
        sa(1, 2)
        vqa(1, 2)
        a(1, 3)
        sa(1, 3)
        vqa(1, 3)
        sinx("B")
        vqx(2, 1)
        tx(3, 0, "S")
        tx(3, 1, "S")
        tx(3, 2, "later")
        vx(3, 2)
        tx(3, 3, "S")
        q(1)
        sn(1, 0)
        sn(1, 1)
        k(2, 0)
        a(2, 0)
        k(2, 1)
        ab(1, 0, 4)
        vk(2, 0)
        ck(1, "G")
        cq(1, 0, 4, "G")
        vk(2, 1)
        store(1, [0, 1], ["q", "kv"])
        sa(2, 0)
        vqa(2, 0)
        a(2, 1)
        sa(2, 1)
        vqa(2, 1)
        vqx(3, 0)
        a(2, 2)
        sa(2, 2)
        vqa(2, 2)
        a(2, 3)
        sa(2, 3)
        vqa(2, 3)
        vqx(3, 1)
        tx(4, 0, "S")
        tx(4, 1, "S")
        tx(4, 2, "later")
        vx(4, 2)
        tx(4, 3, "S")
        q(2)
        sn(2, 0)
        sn(2, 1)
        k(3, 0)
        a(3, 0)
        k(3, 1)
        ab(2, 0, 4)
        vk(3, 0)
        ck(2, "G")
        cq(2, 0, 4, "G")
        vk(3, 1)
        store(2, [0, 1], ["q", "kv"])
        sa(3, 0)
        vqa(3, 0)
        a(3, 1)
        sa(3, 1)
        vqa(3, 1)
        vqx(4, 0)
        a(3, 2)
        sa(3, 2)
        vqa(3, 2)
        a(3, 3)
        sa(3, 3)
        vqa(3, 3)
        vqx(4, 1)
        tx(5, 0, "S")
        tx(5, 1, "S")
        tx(5, 2, "later")
        vx(5, 2)
        tx(5, 3, "S")
        q(3)
        sn(3, 0)
        sn(3, 1)
        k(4, 0)
        a(4, 0)
        k(4, 1)
        ab(3, 0, 4)
        vk(4, 0)
        ck(3, "G")
        cq(3, 0, 4, "G")
        vk(4, 1)
        store(3, [0, 1], ["q", "kv"])
        sa(4, 0)
        vqa(4, 0)
        a(4, 1)
        sa(4, 1)
        vqa(4, 1)
        vqx(5, 0)
        a(4, 2)
        sa(4, 2)
        vqa(4, 2)
        a(4, 3)
        sa(4, 3)
        vqa(4, 3)
        vqx(5, 1)
        tx(6, 0, "S")
        tx(6, 1, "S")
        tx(6, 2, "later")
        vx(6, 2)
        tx(6, 3, "S")
        q(4)
        sn(4, 0)
        sn(4, 1)
        k(5, 0)
        a(5, 0)
        k(5, 1)
        ab(4, 0, 4)
        vk(5, 0)
        ck(4, "G")
        cq(4, 0, 4, "G")
        vk(5, 1)
        store(4, [0, 1], ["q", "kv"])
        sa(5, 0)
        vqa(5, 0)
        a(5, 1)
        sa(5, 1)
        vqa(5, 1)
        vqx(6, 0)
        a(5, 2)
        sa(5, 2)
        vqa(5, 2)
        a(5, 3)
        sa(5, 3)
        vqa(5, 3)
        vqx(6, 1)
        tx(7, 0, "S")
        tx(7, 1, "S")
        tx(7, 2, "later")
        vx(7, 2)
        tx(7, 3, "S")
        q(5)
        sn(5, 0)
        sn(5, 1)
        k(6, 0)
        k(6, 1)
        vqx(7, 0)
        ab(5, 0, 4)
        vk(6, 0)
        ck(5, "G")
        cq(5, 0, 4, "V")
        store(5, [0, 1], ["q", "kv"])
        vqx(7, 1)
        a(6, 0)
        sa(6, 0)
        vqa(6, 0)
        a(6, 1)
        sa(6, 1)
        vk(6, 1)
        vqa(6, 1)
        a(6, 2)
        sa(6, 2)
        vqa(6, 2)
        a(6, 3)
        sa(6, 3)
        vqa(6, 3)
        k(7, 0)
        ck(6, "G")
        store(6, [0, 1], ["kv"])
        a(7, 0)
        sa(7, 0)
        vk(7, 0)
        k(7, 1)
        vqa(7, 0)
        a(7, 1)
        sa(7, 1)
        vk(7, 1)
        qpair(6, 0)
        sn(6, 0)
        ck(7, "G")
        store(7, [0, 1], ["kv"])
        a(7, 2)
        sa(7, 2)
        ab(6, 0, 2)
        vqa(7, 1)
        cq(6, 0, 2, "G")
        store(6, [0], ["q"])
        qpair(6, 1)
        a(7, 3)
        sa(7, 3)
        sn(6, 1)
        ab(6, 2, 2)
        vqa(7, 2)
        cq(6, 2, 2, "V")
        vqa(7, 3)
        store(6, [1], ["q"])
        qpair(7, 0)
        sn(7, 0)
        ab(7, 0, 2)
        cq(7, 0, 2, "V")
        store(7, [0], ["q"])
        qpair(7, 1)
        sn(7, 1)
        ab(7, 2, 2)
        cq(7, 2, 2, "V")
        store(7, [1], ["q"])
